import numpy as np
import ml_dtypes


def mxq(x, axis, fmt="e4m3"):
    dtype, down = {"e4m3": (ml_dtypes.float8_e4m3fn, 7), "e5m2": (ml_dtypes.float8_e5m2, 14)}[fmt]
    v = np.moveaxis(np.asarray(x, np.float32).astype(ml_dtypes.bfloat16).astype(np.float64), axis, -1)
    blocks = v.reshape(v.shape[:-1] + (-1, 32))
    amax = np.abs(blocks).max(-1, keepdims=True)
    byte = np.maximum(np.where(amax > 0, np.frexp(amax)[1] - 1 + 127, 0) - down, 1)
    scale = np.exp2(byte - 127.0)
    codes = (blocks / scale).astype(np.float32).astype(dtype).astype(np.float64)
    return np.moveaxis((codes * scale).reshape(v.shape), -1, axis)


WIDE = False


def mx_kscale(k):
    if not WIDE:
        return np.ones(k)
    levels = np.array([10, -10, 5, -5, 0])
    a = np.random.permutation(np.resize(levels, k // 512 * 4)).reshape(k // 512, 4)
    idx = np.arange(k)
    return np.exp2(a[idx // 512, idx % 128 // 32])


BF16 = ml_dtypes.bfloat16


def bf(x):
    return np.asarray(x, np.float32).astype(BF16)


def f64(x):
    return np.asarray(x).astype(np.float64)


N, D_IN, D_SAE = 8192, 512, 512
NORM_MULT = 8.0
X_MULT = 8.0


def setup_inputs():
    s = mx_kscale(D_IN)
    s = s / s.max()
    t = mx_kscale(D_SAE)
    b = 0.1875 * np.random.standard_normal(D_IN)
    w0 = np.random.standard_normal((D_SAE, D_IN))
    sign = np.sign(np.random.standard_normal(D_SAE))
    return {"x": bf((b + 0.125 * np.random.standard_normal((N, D_IN))) * s),
            "enc_w": bf(w0 * NORM_MULT / np.sqrt(D_IN) * t[:, None] / s),
            "enc_b": bf((0.5 + 2.4 * sign + 0.3 * np.random.standard_normal(D_SAE)) * t),
            "dec_w": bf((w0.T + 0.5 * np.random.standard_normal((D_IN, D_SAE))) * 0.5 * NORM_MULT / np.sqrt(D_SAE) * s[:, None] / t),
            "dec_b": bf(b * s),
            "log_threshold": bf(np.log(0.5) + 0.3 * np.random.standard_normal(D_SAE) + np.log(t))}


def reference(x, enc_w, enc_b, dec_w, dec_b, log_threshold):
    x = f64(x)
    dec_b = f64(dec_b)
    xc = x - dec_b
    h = (mxq(xc, 1, "e4m3") @ mxq(f64(enc_w), 1, "e4m3").T) + f64(enc_b)
    thr = np.exp(f64(log_threshold))
    s = (h > thr).astype(np.float64)
    a = h * s
    recon = ((mxq(a, 1, "e4m3") @ mxq(f64(dec_w), 1, "e4m3").T) + dec_b) / (NORM_MULT ** 2)
    rec_loss = np.mean((recon - x) ** 2, axis=0).sum() / (X_MULT ** 2)
    return s, rec_loss

@@ -1,0 +1,222 @@
+from contextlib import ExitStack
+
+import concourse.mybir as mybir
+from concourse.masks import make_identity
+
+FLOPS = 2 * 2 * 8192 * 512 * 512
+
+F32 = mybir.dt.float32
+BF16 = mybir.dt.bfloat16
+U32 = mybir.dt.uint32
+U8 = mybir.dt.uint8
+FP8X4 = mybir.dt.float8_e4m3fn_x4
+ALU = mybir.AluOpType
+ACT = mybir.ActivationFunctionType
+AX = mybir.AxisListType
+
+P = 128
+D = 512
+TOK = 512
+N_TOK = 8192
+ROUNDS = N_TOK // TOK
+
+
+def as_row(ap):
+    v = ap
+    while v.ndim < 2:
+        v = v.unsqueeze(0)
+    return v
+
+
+def tile_sae_t_kernel(tc, x, enc_w, enc_b, dec_w, dec_b, log_threshold, out_0, out_1):
+    nc = tc.nc
+    with ExitStack() as ctx:
+        consts = ctx.enter_context(tc.tile_pool(name="consts", bufs=1))
+        work = ctx.enter_context(tc.tile_pool(name="work", bufs=2))
+        psum = ctx.enter_context(tc.psum_pool(name="psum", bufs=1))
+
+        ident_f = consts.tile([P, P], F32, name="ident_f")
+        make_identity(nc, ident_f[:])
+        ident_b = consts.tile([P, P], BF16, name="ident_b")
+        make_identity(nc, ident_b[:])
+
+        vb = consts.tile([P, P], BF16, name="vb")
+        nc.vector.memset(vb[:], 0.0)
+        vw = consts.tile([P, 2 * P], BF16, name="vw")
+        nc.vector.memset(vw[:], 0.0)
+        nc.sync.dma_start(out=vw[0:2, :], in_=dec_b.rearrange("(u w) -> u w", u=2))
+        nc.sync.dma_start(out=vb[0:4, :], in_=enc_b.rearrange("(t p) -> t p", p=P))
+        nc.sync.dma_start(out=vb[4:8, :], in_=log_threshold.rearrange("(t p) -> t p", p=P))
+        ew = consts.tile([P, 4 * D], BF16, name="ew")
+        nc.sync.dma_start(
+            out=ew[:].rearrange("r (t k) -> r t k", t=4),
+            in_=enc_w.rearrange("(t r) k -> r t k", r=P),
+        )
+
+        def load_x(m):
+            xs = work.tile([P, 4 * D], BF16, name="xs", tag="xs", bufs=3)
+            nc.sync.dma_start(
+                out=xs[:], in_=x[m * TOK : (m + 1) * TOK, :].rearrange("(p j) k -> p (j k)", j=4)
+            )
+            return xs
+
+        xs_tiles = [load_x(0)]
+        dw = consts.tile([P, 4 * D], BF16, name="dw")
+        nc.sync.dma_start(
+            out=dw[:].rearrange("j (u eh) -> j u eh", u=2),
+            in_=dec_w.rearrange("(u j e) h -> j u (e h)", u=2, e=2),
+        )
+
+        pw = psum.tile([P, P], F32, name="pw", tag="r", bufs=2)
+        nc.tensor.transpose(pw[:], vw[:].bitcast(F32), ident_f[:])
+        decw2 = consts.tile([P, 2], F32, name="decw2")
+        nc.vector.tensor_copy(out=decw2[:], in_=pw[:, 0:2])
+        decb4 = decw2[:].bitcast(BF16)
+        decbf = consts.tile([P, 4], F32, name="decbf")
+        nc.vector.tensor_copy(out=decbf[:], in_=decb4)
+
+        pv = psum.tile([P, P], BF16, name="pv", tag="r", bufs=2)
+        nc.tensor.transpose(pv[:], vb[:], ident_b[:])
+        encb = consts.tile([P, 4], F32, name="encb")
+        nc.vector.tensor_copy(out=encb[:], in_=pv[:, 0:4])
+        thr = consts.tile([P, 4], F32, name="thr")
+        nc.scalar.activation(out=thr[:], in_=pv[:, 4:8], func=ACT.Exp)
+        cthr = consts.tile([P, 4], F32, name="cthr")
+        nc.vector.tensor_tensor(out=cthr[:], in0=thr[:], in1=encb[:], op=ALU.subtract)
+
+        lacc = consts.tile([P, 4 * ROUNDS], F32, name="lacc")
+        ones = consts.tile([P, P], F32, name="ones")
+        nc.vector.memset(ones[:], 2.0 ** -31)
+
+        def words_to_k(src, dst):
+            srcw = src[:].bitcast(F32)
+            dstw = dst[:].bitcast(F32).rearrange("p (j r u) -> p j r u", j=4, u=2)
+            for b in range(2):
+                xt = psum.tile([P, 2, 2, P], F32, name="xt", tag="xt", bufs=1)
+                for jj in range(2):
+                    for u in range(2):
+                        c0 = (2 * b + jj) * 256 + P * u
+                        nc.tensor.transpose(xt[:, jj, u, :], srcw[:, c0 : c0 + P], ident_f[:])
+                nc.scalar.copy(
+                    out=dstw[:, 2 * b : 2 * b + 2, :, :], in_=xt[:].rearrange("p j u r -> p j r u")
+                )
+
+        eg = consts.tile([P, 4 * D], BF16, name="eg", align_bytes=64)
+        words_to_k(ew, eg)
+        enc_q = consts.tile([P, D], U32, name="enc_q", align_bytes=64)
+        enc_s = consts.tile([P, D], U8, name="enc_s", align_bytes=64)
+        nc.vector.quantize_mx(out=enc_q[:].bitcast(FP8X4), scales=enc_s[:], in_=eg[:])
+
+        dg = consts.tile([P, 4 * D], BF16, name="dg", align_bytes=64)
+        dgv = dg[:].rearrange("p (c j t) -> p c j t", c=4, t=4)
+        for cb in range(2):
+            dt = psum.tile([P, 2, 4, P], BF16, name="dt", tag="st", bufs=1)
+            for cc in range(2):
+                for t in range(4):
+                    c0 = (2 * cb + cc) * D + P * t
+                    nc.tensor.transpose(dt[:, cc, t, :], dw[:, c0 : c0 + P], ident_b[:])
+            nc.vector.tensor_copy(
+                out=dgv[:, 2 * cb : 2 * cb + 2, :, :], in_=dt[:].rearrange("p c t j -> p c j t")
+            )
+        dec_q = consts.tile([P, D], U32, name="dec_q", align_bytes=64)
+        dec_s = consts.tile([P, D], U8, name="dec_s", align_bytes=64)
+        nc.vector.quantize_mx(out=dec_q[:].bitcast(FP8X4), scales=dec_s[:], in_=dg[:])
+
+        for m in range(ROUNDS):
+            if m + 1 < ROUNDS:
+                xs_tiles.append(load_x(m + 1))
+            xs = xs_tiles[m]
+            xg = work.tile([P, 4 * TOK], BF16, name="xg", tag="xg", bufs=4, align_bytes=64)
+            words_to_k(xs, xg)
+            xc = work.tile([P, 4 * TOK], BF16, name="xc", tag="xc", bufs=2, align_bytes=64)
+            nc.vector.tensor_tensor(
+                out=xc[:].rearrange("p (c t) -> p c t", t=4),
+                in0=xg[:].rearrange("p (c t) -> p c t", t=4),
+                in1=decb4.unsqueeze(1).to_broadcast([P, TOK, 4]),
+                op=ALU.subtract,
+            )
+            xq = work.tile([P, TOK], U32, name="xq", tag="xq", bufs=2, align_bytes=64)
+            xsc = work.tile([P, TOK], U8, name="xsc", tag="xsc", bufs=2, align_bytes=64)
+            nc.vector.quantize_mx(out=xq[:].bitcast(FP8X4), scales=xsc[:], in_=xc[:])
+
+            ap = work.tile([P, 4 * TOK], BF16, name="ap", tag="ap", bufs=3)
+            for t in range(4):
+                hps = psum.tile([P, TOK], F32, name="hps", tag="h", bufs=4)
+                nc.tensor.matmul_mx(
+                    out=hps[:],
+                    lhsT=enc_q[:, t * P : (t + 1) * P].bitcast(FP8X4),
+                    lhsT_scale=enc_s[:, t * P : (t + 1) * P],
+                    rhs=xq[:].bitcast(FP8X4),
+                    rhs_scale=xsc[:],
+                    start=True,
+                    stop=True,
+                )
+                hb = work.tile([P, TOK], BF16, name="hb", tag="hb", bufs=4)
+                nc.scalar.activation(out=hb[:], in_=hps[:], func=ACT.Relu, bias=encb[:, t : t + 1], scale=1.0)
+                nc.vector.scalar_tensor_tensor(
+                    out=ap[:, t * TOK : (t + 1) * TOK],
+                    in0=hps[:],
+                    scalar=cthr[:, t : t + 1],
+                    in1=hb[:],
+                    op0=ALU.is_gt,
+                    op1=ALU.mult,
+                )
+            ag = work.tile([P, 4 * TOK], BF16, name="ag", tag="ag", bufs=2, align_bytes=64)
+            nc.vector.tensor_copy(
+                out=ag[:].rearrange("p (c i t) -> p c t i", i=4, t=4),
+                in_=ap[:].rearrange("p (t c i) -> p c t i", t=4, i=4),
+            )
+            aq = work.tile([P, TOK], U32, name="aq", tag="aq", bufs=2, align_bytes=64)
+            asc = work.tile([P, TOK], U8, name="asc", tag="asc", bufs=2, align_bytes=64)
+            nc.vector.quantize_mx(out=aq[:].bitcast(FP8X4), scales=asc[:], in_=ag[:])
+
+            ssb = work.tile([P, 4 * D], F32, name="ssb", tag="ssb", bufs=3)
+            for b in range(2):
+                st = psum.tile([P, 2, D], BF16, name="st", tag="st", bufs=1)
+                for jj in range(2):
+                    for t in range(4):
+                        c0 = t * TOK + (2 * b + jj) * P
+                        nc.tensor.transpose(st[:, jj, t * P : (t + 1) * P], ap[:, c0 : c0 + P], ident_b[:])
+                nc.scalar.activation(
+                    out=ssb[:, 2 * b * D : (2 * b + 2) * D],
+                    in_=st[:].rearrange("p j h -> p (j h)"),
+                    func=ACT.Sign,
+                )
+            nc.sync.dma_start(
+                out=out_0[m * TOK : (m + 1) * TOK, :].rearrange("(p j) h -> p (j h)", j=4), in_=ssb[:]
+            )
+            xgv = xg[:].rearrange("p (c t) -> p c t", t=4)
+            for c in range(4):
+                rps = psum.tile([P, TOK], F32, name="rps", tag="r", bufs=2)
+                nc.tensor.matmul_mx(
+                    out=rps[:],
+                    lhsT=dec_q[:, c * P : (c + 1) * P].bitcast(FP8X4),
+                    lhsT_scale=dec_s[:, c * P : (c + 1) * P],
+                    rhs=aq[:].bitcast(FP8X4),
+                    rhs_scale=asc[:],
+                    start=True,
+                    stop=True,
+                )
+                d0 = work.tile([P, TOK], F32, name="d0", tag="d0", bufs=4)
+                nc.vector.scalar_tensor_tensor(
+                    out=d0[:],
+                    in0=xgv[:, :, c],
+                    scalar=-64.0,
+                    in1=rps[:],
+                    op0=ALU.mult,
+                    op1=ALU.add,
+                )
+                nc.scalar.activation(
+                    out=d0[:],
+                    in_=d0[:],
+                    func=ACT.Square,
+                    bias=decbf[:, c : c + 1],
+                    scale=1.0,
+                    accum_out=lacc[:, 4 * m + c : 4 * m + c + 1],
+                )
+
+        pl = psum.tile([P, 4 * ROUNDS], F32, name="pl", tag="r", bufs=2)
+        nc.tensor.matmul(pl[:], lhsT=ones[:], rhs=lacc[:], start=True, stop=True)
+        tot = consts.tile([P, 1], F32, name="tot")
+        nc.vector.tensor_reduce(out=tot[:], in_=pl[:], axis=AX.X, op=ALU.add)
+        nc.sync.dma_start(out=as_row(out_1), in_=tot[0:1, 0:1])

@@ -33,189 +33,311 @@ def tile_sae_t_kernel(tc, x, enc_w, enc_b, dec_w, dec_b, log_threshold, out_0, o
     with ExitStack() as ctx:
         consts = ctx.enter_context(tc.tile_pool(name="consts", bufs=1))
         work = ctx.enter_context(tc.tile_pool(name="work", bufs=2))
-        psum = ctx.enter_context(tc.psum_pool(name="psum", bufs=1))
+        psum = ctx.enter_context(tc.psum_pool(name="psum", bufs=2))
+        ctx.enter_context(tc.manual_schedule())
 
+        xs_t, xt_t, xg_t, xc_t, xq_t, h_t, hf_t = {}, {}, {}, {}, {}, {}, {}
+        ap_t, ag_t, aq_t, st_t, ss_t, r_t, d_t = {}, {}, {}, {}, {}, {}, {}
+
+        def live(q):
+            return 0 <= q < ROUNDS
+
+        def load(q):
+            if live(q):
+                xs_t[q] = work.tile([P, 4 * D], BF16, name="xs", tag="xs", bufs=4)
+                nc.sync.dma_start(
+                    out=xs_t[q][:], in_=x[q * TOK : (q + 1) * TOK, :].rearrange("(p j) k -> p (j k)", j=4)
+                )
+
+        warm = consts.tile([P, 1], F32, name="warm")
+        nc.vector.memset(warm[:], 0.0)
+        warm2 = consts.tile([P, 1], F32, name="warm2")
+        nc.scalar.activation(out=warm2[:], in_=warm[:], func=ACT.Exp)
+        vb = consts.tile([P, P], BF16, name="vb")
+        nc.vector.memset(vb[:], 0.0)
+        vw = consts.tile([P, 2 * P], BF16, name="vw")
+        nc.vector.memset(vw[:], 0.0)
+        ones = consts.tile([P, P], F32, name="ones")
+        nc.vector.memset(ones[:], 2.0 ** -31)
         ident_f = consts.tile([P, P], F32, name="ident_f")
         make_identity(nc, ident_f[:])
         ident_b = consts.tile([P, P], BF16, name="ident_b")
         make_identity(nc, ident_b[:])
 
-        vb = consts.tile([P, P], BF16, name="vb")
-        nc.vector.memset(vb[:], 0.0)
-        vw = consts.tile([P, 2 * P], BF16, name="vw")
-        nc.vector.memset(vw[:], 0.0)
         nc.sync.dma_start(out=vw[0:2, :], in_=dec_b.rearrange("(u w) -> u w", u=2))
-        nc.sync.dma_start(out=vb[0:4, :], in_=enc_b.rearrange("(t p) -> t p", p=P))
-        nc.sync.dma_start(out=vb[4:8, :], in_=log_threshold.rearrange("(t p) -> t p", p=P))
+        load(0)
         ew = consts.tile([P, 4 * D], BF16, name="ew")
         nc.sync.dma_start(
             out=ew[:].rearrange("r (t k) -> r t k", t=4),
             in_=enc_w.rearrange("(t r) k -> r t k", r=P),
         )
-
-        def load_x(m):
-            xs = work.tile([P, 4 * D], BF16, name="xs", tag="xs", bufs=3)
-            nc.sync.dma_start(
-                out=xs[:], in_=x[m * TOK : (m + 1) * TOK, :].rearrange("(p j) k -> p (j k)", j=4)
-            )
-            return xs
-
-        xs_tiles = [load_x(0)]
+        load(1)
+        nc.sync.dma_start(out=vb[0:4, :], in_=enc_b.rearrange("(t p) -> t p", p=P))
+        nc.sync.dma_start(out=vb[4:8, :], in_=log_threshold.rearrange("(t p) -> t p", p=P))
         dw = consts.tile([P, 4 * D], BF16, name="dw")
         nc.sync.dma_start(
             out=dw[:].rearrange("j (u eh) -> j u eh", u=2),
             in_=dec_w.rearrange("(u j e) h -> j u (e h)", u=2, e=2),
         )
+        load(2)
+        load(3)
 
-        pw = psum.tile([P, P], F32, name="pw", tag="r", bufs=2)
+        pw = psum.tile([P, P], F32, name="pw", tag="r")
         nc.tensor.transpose(pw[:], vw[:].bitcast(F32), ident_f[:])
         decw2 = consts.tile([P, 2], F32, name="decw2")
         nc.vector.tensor_copy(out=decw2[:], in_=pw[:, 0:2])
         decb4 = decw2[:].bitcast(BF16)
         decbf = consts.tile([P, 4], F32, name="decbf")
         nc.vector.tensor_copy(out=decbf[:], in_=decb4)
-
-        pv = psum.tile([P, P], BF16, name="pv", tag="r", bufs=2)
-        nc.tensor.transpose(pv[:], vb[:], ident_b[:])
-        encb = consts.tile([P, 4], F32, name="encb")
-        nc.vector.tensor_copy(out=encb[:], in_=pv[:, 0:4])
-        thr = consts.tile([P, 4], F32, name="thr")
-        nc.scalar.activation(out=thr[:], in_=pv[:, 4:8], func=ACT.Exp)
-        cthr = consts.tile([P, 4], F32, name="cthr")
-        nc.vector.tensor_tensor(out=cthr[:], in0=thr[:], in1=encb[:], op=ALU.subtract)
-
         lacc = consts.tile([P, 4 * ROUNDS], F32, name="lacc")
-        ones = consts.tile([P, P], F32, name="ones")
-        nc.vector.memset(ones[:], 2.0 ** -31)
-
-        def words_to_k(src, dst):
-            srcw = src[:].bitcast(F32)
-            dstw = dst[:].bitcast(F32).rearrange("p (j r u) -> p j r u", j=4, u=2)
-            for b in range(2):
-                xt = psum.tile([P, 2, 2, P], F32, name="xt", tag="xt", bufs=1)
-                for jj in range(2):
-                    for u in range(2):
-                        c0 = (2 * b + jj) * 256 + P * u
-                        nc.tensor.transpose(xt[:, jj, u, :], srcw[:, c0 : c0 + P], ident_f[:])
-                nc.scalar.copy(
-                    out=dstw[:, 2 * b : 2 * b + 2, :, :], in_=xt[:].rearrange("p j u r -> p j r u")
-                )
-
-        eg = consts.tile([P, 4 * D], BF16, name="eg", align_bytes=64)
-        words_to_k(ew, eg)
+        encb = consts.tile([P, 4], F32, name="encb")
+        thr = consts.tile([P, 4], F32, name="thr")
         enc_q = consts.tile([P, D], U32, name="enc_q", align_bytes=64)
         enc_s = consts.tile([P, D], U8, name="enc_s", align_bytes=64)
-        nc.vector.quantize_mx(out=enc_q[:].bitcast(FP8X4), scales=enc_s[:], in_=eg[:])
-
+        dec_q = consts.tile([P, D], U32, name="dec_q", align_bytes=64)
+        dec_s = consts.tile([P, D], U8, name="dec_s", align_bytes=64)
+        eg = consts.tile([P, 4 * D], BF16, name="eg", align_bytes=64)
         dg = consts.tile([P, 4 * D], BF16, name="dg", align_bytes=64)
-        dgv = dg[:].rearrange("p (c j t) -> p c j t", c=4, t=4)
+
+        def word_transposes(src, b, bank):
+            srcw = src[:].bitcast(F32)
+            for jj in range(2):
+                for u in range(2):
+                    c0 = (2 * b + jj) * 256 + P * u
+                    nc.tensor.transpose(bank[:, jj, u, :], srcw[:, c0 : c0 + P], ident_f[:])
+
+        def words_out(copy, bank, dst, b):
+            dstw = dst[:].bitcast(F32).rearrange("p (j r u) -> p j r u", j=4, u=2)
+            copy(out=dstw[:, 2 * b : 2 * b + 2, :, :], in_=bank[:].rearrange("p j u r -> p j r u"))
+
+        def x_transposes(q, b):
+            if live(q):
+                xt_t[q, b] = psum.tile([P, 2, 2, P], F32, name="xt", tag="xt")
+                word_transposes(xs_t[q], b, xt_t[q, b])
+
+        def x_out(q, b):
+            if live(q):
+                if b == 0:
+                    xg_t[q] = work.tile([P, 4 * TOK], BF16, name="xg", tag="xg", bufs=6, align_bytes=64)
+                words_out(nc.scalar.copy, xt_t[q, b], xg_t[q], b)
+
+        def centre(q):
+            if live(q):
+                xc_t[q] = work.tile([P, 4 * TOK], BF16, name="xc", tag="xc", bufs=2, align_bytes=64)
+                nc.vector.tensor_tensor(
+                    out=xc_t[q][:].rearrange("p (c t) -> p c t", t=4),
+                    in0=xg_t[q][:].rearrange("p (c t) -> p c t", t=4),
+                    in1=decb4.unsqueeze(1).to_broadcast([P, TOK, 4]),
+                    op=ALU.subtract,
+                )
+
+        def quantise(src, tag):
+            codes = work.tile([P, TOK], U32, name=tag + "_codes", tag=tag + "_codes", bufs=3, align_bytes=64)
+            scales = work.tile([P, TOK], U8, name=tag + "_scales", tag=tag + "_scales", bufs=3, align_bytes=64)
+            nc.vector.quantize_mx(out=codes[:].bitcast(FP8X4), scales=scales[:], in_=src[:])
+            return codes, scales
+
+        def quantise_x(q):
+            if live(q):
+                xq_t[q] = quantise(xc_t[q], "x")
+
+        def mx(bank, w_q, w_s, i, moving):
+            nc.tensor.matmul_mx(
+                out=bank[:],
+                lhsT=w_q[:, i * P : (i + 1) * P].bitcast(FP8X4),
+                lhsT_scale=w_s[:, i * P : (i + 1) * P],
+                rhs=moving[0][:].bitcast(FP8X4),
+                rhs_scale=moving[1][:],
+                start=True,
+                stop=True,
+            )
+
+        def encode(q, t):
+            if live(q):
+                h_t[q, t] = psum.tile([P, TOK], F32, name="hps", tag="h")
+                mx(h_t[q, t], enc_q, enc_s, t, xq_t[q])
+
+        def h_out(q, t):
+            if live(q):
+                hf_t[q, t] = work.tile([P, TOK], F32, name="hf", tag="hf", bufs=8)
+                nc.scalar.activation(
+                    out=hf_t[q, t][:], in_=h_t[q, t][:], func=ACT.Relu, bias=encb[:, t : t + 1], scale=1.0
+                )
+
+        def jump(q, t):
+            if live(q):
+                if t == 0:
+                    ap_t[q] = work.tile([P, 4 * TOK], BF16, name="ap", tag="ap", bufs=3)
+                nc.vector.scalar_tensor_tensor(
+                    out=ap_t[q][:, t * TOK : (t + 1) * TOK],
+                    in0=hf_t[q, t][:],
+                    scalar=thr[:, t : t + 1],
+                    in1=hf_t[q, t][:],
+                    op0=ALU.is_gt,
+                    op1=ALU.mult,
+                )
+
+        def regroup(q):
+            if live(q):
+                ag_t[q] = work.tile([P, 4 * TOK], BF16, name="ag", tag="ag", bufs=2, align_bytes=64)
+                nc.vector.tensor_copy(
+                    out=ag_t[q][:].rearrange("p (c i t) -> p c t i", i=4, t=4),
+                    in_=ap_t[q][:].rearrange("p (t c i) -> p c t i", t=4, i=4),
+                )
+
+        def quantise_a(q):
+            if live(q):
+                aq_t[q] = quantise(ag_t[q], "a")
+
+        def a_transposes(q, b):
+            if live(q):
+                st_t[q, b] = psum.tile([P, 2, D], BF16, name="st", tag="st")
+                for jj in range(2):
+                    for t in range(4):
+                        c0 = t * TOK + (2 * b + jj) * P
+                        nc.tensor.transpose(
+                            st_t[q, b][:, jj, t * P : (t + 1) * P], ap_t[q][:, c0 : c0 + P], ident_b[:]
+                        )
+
+        def s_out(q, b):
+            if live(q):
+                if b == 0:
+                    ss_t[q] = work.tile([P, 4 * D], F32, name="ssb", tag="ssb", bufs=3)
+                s_half = ss_t[q][:, 2 * b * D : (2 * b + 2) * D]
+                a_half = st_t[q, b][:].rearrange("p j h -> p (j h)")
+                if q == ROUNDS - 1 and b == 1:
+                    nc.vector.tensor_single_scalar(out=s_half, in_=a_half, scalar=0.0, op=ALU.is_gt)
+                else:
+                    nc.scalar.activation(out=s_half, in_=a_half, func=ACT.Sign)
+                if b == 1:
+                    nc.sync.dma_start(
+                        out=out_0[q * TOK : (q + 1) * TOK, :].rearrange("(p j) h -> p (j h)", j=4),
+                        in_=ss_t[q][:],
+                    )
+
+        def decode(q, c):
+            if live(q):
+                spare = q >= ROUNDS - 3 and c >= 2
+                r_t[q, c] = psum.tile([P, TOK], F32, name="rps", tag="xt" if spare else "r")
+                mx(r_t[q, c], dec_q, dec_s, c, aq_t[q])
+
+        def residual(q, c):
+            if live(q):
+                d_t[q, c] = work.tile([P, TOK], F32, name="d0", tag="d0", bufs=8)
+                nc.vector.scalar_tensor_tensor(
+                    out=d_t[q, c][:],
+                    in0=xg_t[q][:].rearrange("p (c t) -> p c t", t=4)[:, :, c],
+                    scalar=-64.0,
+                    in1=r_t[q, c][:],
+                    op0=ALU.mult,
+                    op1=ALU.add,
+                )
+
+        def square(q, c):
+            if live(q):
+                nc.scalar.activation(
+                    out=d_t[q, c][:],
+                    in_=d_t[q, c][:],
+                    func=ACT.Square,
+                    bias=decbf[:, c : c + 1],
+                    scale=1.0,
+                    accum_out=lacc[:, 4 * q + c : 4 * q + c + 1],
+                )
+
+        x_transposes(0, 0)
+        x_transposes(0, 1)
+        e_banks = []
+        for b in range(2):
+            et = psum.tile([P, 2, 2, P], F32, name="et", tag="h")
+            word_transposes(ew, b, et)
+            e_banks.append(et)
+        x_out(0, 0)
+        x_out(0, 1)
+        for b in range(2):
+            words_out(nc.scalar.copy, e_banks[b], eg, b)
+        x_transposes(1, 0)
+        x_transposes(1, 1)
+        pv = psum.tile([P, P], BF16, name="pv", tag="r")
+        nc.tensor.transpose(pv[:], vb[:], ident_b[:])
+        centre(0)
+        quantise_x(0)
+        nc.vector.quantize_mx(out=enc_q[:].bitcast(FP8X4), scales=enc_s[:], in_=eg[:])
+        x_out(1, 0)
+        x_out(1, 1)
+        nc.vector.tensor_copy(out=encb[:], in_=pv[:, 0:4])
+        nc.scalar.activation(out=thr[:], in_=pv[:, 4:8], func=ACT.Exp)
+        encode(0, 0)
+        encode(0, 1)
+        d_banks = []
         for cb in range(2):
-            dt = psum.tile([P, 2, 4, P], BF16, name="dt", tag="st", bufs=1)
+            dt = psum.tile([P, 2, 4, P], BF16, name="dt", tag="st")
             for cc in range(2):
                 for t in range(4):
                     c0 = (2 * cb + cc) * D + P * t
                     nc.tensor.transpose(dt[:, cc, t, :], dw[:, c0 : c0 + P], ident_b[:])
-            nc.vector.tensor_copy(
-                out=dgv[:, 2 * cb : 2 * cb + 2, :, :], in_=dt[:].rearrange("p c t j -> p c j t")
-            )
-        dec_q = consts.tile([P, D], U32, name="dec_q", align_bytes=64)
-        dec_s = consts.tile([P, D], U8, name="dec_s", align_bytes=64)
+            d_banks.append(dt)
+        x_transposes(2, 0)
+        x_transposes(2, 1)
+        dgv = dg[:].rearrange("p (c j t) -> p c j t", c=4, t=4)
+        centre(1)
+        nc.vector.tensor_copy(out=dgv[:, 0:2, :, :], in_=d_banks[0][:].rearrange("p c t j -> p c j t"))
+        quantise_x(1)
+        nc.vector.tensor_copy(out=dgv[:, 2:4, :, :], in_=d_banks[1][:].rearrange("p c t j -> p c j t"))
+        x_out(2, 0)
+        x_out(2, 1)
+        x_transposes(3, 0)
         nc.vector.quantize_mx(out=dec_q[:].bitcast(FP8X4), scales=dec_s[:], in_=dg[:])
 
-        for m in range(ROUNDS):
-            if m + 1 < ROUNDS:
-                xs_tiles.append(load_x(m + 1))
-            xs = xs_tiles[m]
-            xg = work.tile([P, 4 * TOK], BF16, name="xg", tag="xg", bufs=4, align_bytes=64)
-            words_to_k(xs, xg)
-            xc = work.tile([P, 4 * TOK], BF16, name="xc", tag="xc", bufs=2, align_bytes=64)
-            nc.vector.tensor_tensor(
-                out=xc[:].rearrange("p (c t) -> p c t", t=4),
-                in0=xg[:].rearrange("p (c t) -> p c t", t=4),
-                in1=decb4.unsqueeze(1).to_broadcast([P, TOK, 4]),
-                op=ALU.subtract,
-            )
-            xq = work.tile([P, TOK], U32, name="xq", tag="xq", bufs=2, align_bytes=64)
-            xsc = work.tile([P, TOK], U8, name="xsc", tag="xsc", bufs=2, align_bytes=64)
-            nc.vector.quantize_mx(out=xq[:].bitcast(FP8X4), scales=xsc[:], in_=xc[:])
-
-            ap = work.tile([P, 4 * TOK], BF16, name="ap", tag="ap", bufs=3)
+        for q in range(-1, ROUNDS + 2):
+            draining = q >= ROUNDS - 1
+            if q + 5 >= 4:
+                load(q + 5)
+            square(q - 2, 2)
+            square(q - 2, 3)
             for t in range(4):
-                hps = psum.tile([P, TOK], F32, name="hps", tag="h", bufs=4)
-                nc.tensor.matmul_mx(
-                    out=hps[:],
-                    lhsT=enc_q[:, t * P : (t + 1) * P].bitcast(FP8X4),
-                    lhsT_scale=enc_s[:, t * P : (t + 1) * P],
-                    rhs=xq[:].bitcast(FP8X4),
-                    rhs_scale=xsc[:],
-                    start=True,
-                    stop=True,
-                )
-                hb = work.tile([P, TOK], BF16, name="hb", tag="hb", bufs=4)
-                nc.scalar.activation(out=hb[:], in_=hps[:], func=ACT.Relu, bias=encb[:, t : t + 1], scale=1.0)
-                nc.vector.scalar_tensor_tensor(
-                    out=ap[:, t * TOK : (t + 1) * TOK],
-                    in0=hps[:],
-                    scalar=cthr[:, t : t + 1],
-                    in1=hb[:],
-                    op0=ALU.is_gt,
-                    op1=ALU.mult,
-                )
-            ag = work.tile([P, 4 * TOK], BF16, name="ag", tag="ag", bufs=2, align_bytes=64)
-            nc.vector.tensor_copy(
-                out=ag[:].rearrange("p (c i t) -> p c t i", i=4, t=4),
-                in_=ap[:].rearrange("p (t c i) -> p c t i", t=4, i=4),
-            )
-            aq = work.tile([P, TOK], U32, name="aq", tag="aq", bufs=2, align_bytes=64)
-            asc = work.tile([P, TOK], U8, name="asc", tag="asc", bufs=2, align_bytes=64)
-            nc.vector.quantize_mx(out=aq[:].bitcast(FP8X4), scales=asc[:], in_=ag[:])
+                jump(q, t)
+            h_out(q + 1, 0)
+            encode(q + 1, 2)
+            s_out(q - 1, 0)
+            h_out(q + 1, 1)
+            encode(q + 1, 3)
+            regroup(q)
+            residual(q - 1, 0)
+            decode(q - 1, 2)
+            quantise_a(q)
+            residual(q - 1, 1)
+            decode(q - 1, 3)
+            if q >= 0:
+                x_out(q + 3, 0)
+            h_out(q + 1, 2)
+            square(q - 1, 0)
+            h_out(q + 1, 3)
+            if q >= 0:
+                x_transposes(q + 3, 1)
+            if draining:
+                decode(q, 0)
+                decode(q, 1)
+            a_transposes(q, 0)
+            if q >= 0:
+                x_transposes(q + 4, 0)
+            s_out(q - 1, 1)
+            a_transposes(q, 1)
+            if q >= 0:
+                centre(q + 2)
+            residual(q - 1, 2)
+            if q >= 0:
+                quantise_x(q + 2)
+            residual(q - 1, 3)
+            square(q - 1, 1)
+            if q >= 0:
+                x_out(q + 3, 1)
+            encode(q + 2, 0)
+            encode(q + 2, 1)
+            if not draining:
+                decode(q, 0)
+                decode(q, 1)
 
-            ssb = work.tile([P, 4 * D], F32, name="ssb", tag="ssb", bufs=3)
-            for b in range(2):
-                st = psum.tile([P, 2, D], BF16, name="st", tag="st", bufs=1)
-                for jj in range(2):
-                    for t in range(4):
-                        c0 = t * TOK + (2 * b + jj) * P
-                        nc.tensor.transpose(st[:, jj, t * P : (t + 1) * P], ap[:, c0 : c0 + P], ident_b[:])
-                nc.scalar.activation(
-                    out=ssb[:, 2 * b * D : (2 * b + 2) * D],
-                    in_=st[:].rearrange("p j h -> p (j h)"),
-                    func=ACT.Sign,
-                )
-            nc.sync.dma_start(
-                out=out_0[m * TOK : (m + 1) * TOK, :].rearrange("(p j) h -> p (j h)", j=4), in_=ssb[:]
-            )
-            xgv = xg[:].rearrange("p (c t) -> p c t", t=4)
-            for c in range(4):
-                rps = psum.tile([P, TOK], F32, name="rps", tag="r", bufs=2)
-                nc.tensor.matmul_mx(
-                    out=rps[:],
-                    lhsT=dec_q[:, c * P : (c + 1) * P].bitcast(FP8X4),
-                    lhsT_scale=dec_s[:, c * P : (c + 1) * P],
-                    rhs=aq[:].bitcast(FP8X4),
-                    rhs_scale=asc[:],
-                    start=True,
-                    stop=True,
-                )
-                d0 = work.tile([P, TOK], F32, name="d0", tag="d0", bufs=4)
-                nc.vector.scalar_tensor_tensor(
-                    out=d0[:],
-                    in0=xgv[:, :, c],
-                    scalar=-64.0,
-                    in1=rps[:],
-                    op0=ALU.mult,
-                    op1=ALU.add,
-                )
-                nc.scalar.activation(
-                    out=d0[:],
-                    in_=d0[:],
-                    func=ACT.Square,
-                    bias=decbf[:, c : c + 1],
-                    scale=1.0,
-                    accum_out=lacc[:, 4 * m + c : 4 * m + c + 1],
-                )
-
-        pl = psum.tile([P, 4 * ROUNDS], F32, name="pl", tag="r", bufs=2)
+        pl = psum.tile([P, 4 * ROUNDS], F32, name="pl", tag="r")
         nc.tensor.matmul(pl[:], lhsT=ones[:], rhs=lacc[:], start=True, stop=True)
         tot = consts.tile([P, 1], F32, name="tot")
         nc.vector.tensor_reduce(out=tot[:], in_=pl[:], axis=AX.X, op=ALU.add)

@@ -115,11 +115,11 @@ def tile_sae_t_kernel(tc, x, enc_w, enc_b, dec_w, dec_b, log_threshold, out_0, o
                 xt_t[q, b] = psum.tile([P, 2, 2, P], F32, name="xt", tag="xt")
                 word_transposes(xs_t[q], b, xt_t[q, b])
 
-        def x_out(q, b):
+        def x_out(q, b, copy=nc.scalar.copy):
             if live(q):
                 if b == 0:
                     xg_t[q] = work.tile([P, 4 * TOK], BF16, name="xg", tag="xg", bufs=6, align_bytes=64)
-                words_out(nc.scalar.copy, xt_t[q, b], xg_t[q], b)
+                words_out(copy, xt_t[q, b], xg_t[q], b)
 
         def centre(q):
             if live(q):
@@ -252,7 +252,7 @@ def tile_sae_t_kernel(tc, x, enc_w, enc_b, dec_w, dec_b, log_threshold, out_0, o
             word_transposes(ew, b, et)
             e_banks.append(et)
         x_out(0, 0)
-        x_out(0, 1)
+        x_out(0, 1, nc.vector.tensor_copy)
         for b in range(2):
             words_out(nc.scalar.copy, e_banks[b], eg, b)
         x_transposes(1, 0)
@@ -266,8 +266,6 @@ def tile_sae_t_kernel(tc, x, enc_w, enc_b, dec_w, dec_b, log_threshold, out_0, o
         x_out(1, 1)
         nc.vector.tensor_copy(out=encb[:], in_=pv[:, 0:4])
         nc.scalar.activation(out=thr[:], in_=pv[:, 4:8], func=ACT.Exp)
-        encode(0, 0)
-        encode(0, 1)
         d_banks = []
         for cb in range(2):
             dt = psum.tile([P, 2, 4, P], BF16, name="dt", tag="st")
@@ -276,66 +274,93 @@ def tile_sae_t_kernel(tc, x, enc_w, enc_b, dec_w, dec_b, log_threshold, out_0, o
                     c0 = (2 * cb + cc) * D + P * t
                     nc.tensor.transpose(dt[:, cc, t, :], dw[:, c0 : c0 + P], ident_b[:])
             d_banks.append(dt)
+        encode(0, 0)
+        encode(0, 1)
         x_transposes(2, 0)
         x_transposes(2, 1)
         dgv = dg[:].rearrange("p (c j t) -> p c j t", c=4, t=4)
         centre(1)
-        nc.vector.tensor_copy(out=dgv[:, 0:2, :, :], in_=d_banks[0][:].rearrange("p c t j -> p c j t"))
+        nc.scalar.copy(out=dgv[:, 0:2, :, :], in_=d_banks[0][:].rearrange("p c t j -> p c j t"))
         quantise_x(1)
-        nc.vector.tensor_copy(out=dgv[:, 2:4, :, :], in_=d_banks[1][:].rearrange("p c t j -> p c j t"))
+        nc.scalar.copy(out=dgv[:, 2:4, :, :], in_=d_banks[1][:].rearrange("p c t j -> p c j t"))
         x_out(2, 0)
         x_out(2, 1)
         x_transposes(3, 0)
+        centre(2)
         nc.vector.quantize_mx(out=dec_q[:].bitcast(FP8X4), scales=dec_s[:], in_=dg[:])
+        quantise_x(2)
 
-        for q in range(-1, ROUNDS + 2):
-            draining = q >= ROUNDS - 1
-            if q + 5 >= 4:
-                load(q + 5)
+        def steady(q):
             square(q - 2, 2)
             square(q - 2, 3)
             for t in range(4):
                 jump(q, t)
-            h_out(q + 1, 0)
-            encode(q + 1, 2)
-            s_out(q - 1, 0)
-            h_out(q + 1, 1)
-            encode(q + 1, 3)
-            regroup(q)
-            residual(q - 1, 0)
-            decode(q - 1, 2)
-            quantise_a(q)
-            residual(q - 1, 1)
-            decode(q - 1, 3)
-            if q >= 0:
-                x_out(q + 3, 0)
-            h_out(q + 1, 2)
-            square(q - 1, 0)
-            h_out(q + 1, 3)
             if q >= 0:
                 x_transposes(q + 3, 1)
-            if draining:
-                decode(q, 0)
-                decode(q, 1)
+            s_out(q - 1, 0)
+            h_out(q + 1, 0)
+            h_out(q + 1, 1)
+            residual(q - 1, 0)
+            decode(q - 1, 2)
+            residual(q - 1, 1)
+            decode(q - 1, 3)
+            encode(q + 1, 2)
+            s_out(q - 1, 1)
+            regroup(q)
+            if q >= 1:
+                centre(q + 2)
+            quantise_a(q)
+            if q >= 0:
+                x_out(q + 3, 0)
+            encode(q + 1, 3)
             a_transposes(q, 0)
             if q >= 0:
                 x_transposes(q + 4, 0)
-            s_out(q - 1, 1)
+            square(q - 1, 0)
             a_transposes(q, 1)
-            if q >= 0:
-                centre(q + 2)
+            h_out(q + 1, 2)
+            h_out(q + 1, 3)
             residual(q - 1, 2)
-            if q >= 0:
+            if q >= 1:
                 quantise_x(q + 2)
             residual(q - 1, 3)
             square(q - 1, 1)
             if q >= 0:
                 x_out(q + 3, 1)
             encode(q + 2, 0)
+            decode(q, 0)
             encode(q + 2, 1)
-            if not draining:
-                decode(q, 0)
-                decode(q, 1)
+            decode(q, 1)
+
+        def drain(q):
+            square(q - 2, 2)
+            square(q - 2, 3)
+            for t in range(4):
+                jump(q, t)
+            residual(q - 1, 0)
+            s_out(q - 1, 0)
+            regroup(q)
+            decode(q - 1, 2)
+            residual(q - 1, 1)
+            quantise_a(q)
+            s_out(q - 1, 1)
+            decode(q - 1, 3)
+            square(q - 1, 0)
+            a_transposes(q, 0)
+            decode(q, 0)
+            decode(q, 1)
+            a_transposes(q, 1)
+            residual(q - 1, 2)
+            residual(q - 1, 3)
+            square(q - 1, 1)
+
+        for q in range(-1, ROUNDS + 2):
+            if q + 5 >= 4:
+                load(q + 5)
+            if q < ROUNDS - 1:
+                steady(q)
+            else:
+                drain(q)
 
         pl = psum.tile([P, 4 * ROUNDS], F32, name="pl", tag="r")
         nc.tensor.matmul(pl[:], lhsT=ones[:], rhs=lacc[:], start=True, stop=True)

@@ -154,7 +154,7 @@ def tile_sae_t_kernel(tc, x, enc_w, enc_b, dec_w, dec_b, log_threshold, out_0, o
 
         def encode(q, t):
             if live(q):
-                h_t[q, t] = psum.tile([P, TOK], F32, name="hps", tag="h")
+                h_t[q, t] = psum.tile([P, TOK], F32, name="hps", tag="r" if q == 0 and t >= 2 else "h")
                 mx(h_t[q, t], enc_q, enc_s, t, xq_t[q])
 
         def h_out(q, t):
@@ -244,59 +244,153 @@ def tile_sae_t_kernel(tc, x, enc_w, enc_b, dec_w, dec_b, log_threshold, out_0, o
                     accum_out=lacc[:, 4 * q + c : 4 * q + c + 1],
                 )
 
-        x_transposes(0, 0)
-        x_transposes(0, 1)
         e_banks = []
-        for b in range(2):
+        d_banks = []
+        pv = psum.tile([P, P], BF16, name="pv", tag="r")
+        dgv = dg[:].rearrange("p (c j t) -> p c j t", c=4, t=4)
+
+        def enc_transposes(b):
             et = psum.tile([P, 2, 2, P], F32, name="et", tag="h")
             word_transposes(ew, b, et)
             e_banks.append(et)
-        x_out(0, 0)
-        x_out(0, 1, nc.vector.tensor_copy)
-        for b in range(2):
+
+        def enc_out(b):
             words_out(nc.scalar.copy, e_banks[b], eg, b)
-        x_transposes(1, 0)
-        x_transposes(1, 1)
-        pv = psum.tile([P, P], BF16, name="pv", tag="r")
-        nc.tensor.transpose(pv[:], vb[:], ident_b[:])
-        centre(0)
-        quantise_x(0)
-        nc.vector.quantize_mx(out=enc_q[:].bitcast(FP8X4), scales=enc_s[:], in_=eg[:])
-        x_out(1, 0)
-        x_out(1, 1)
-        nc.vector.tensor_copy(out=encb[:], in_=pv[:, 0:4])
-        nc.scalar.activation(out=thr[:], in_=pv[:, 4:8], func=ACT.Exp)
-        d_banks = []
-        for cb in range(2):
+
+        def quantise_enc():
+            nc.vector.quantize_mx(out=enc_q[:].bitcast(FP8X4), scales=enc_s[:], in_=eg[:])
+
+        def vector_transpose():
+            nc.tensor.transpose(pv[:], vb[:], ident_b[:])
+
+        def enc_b_out():
+            nc.vector.tensor_copy(out=encb[:], in_=pv[:, 0:4])
+
+        def threshold():
+            nc.scalar.activation(out=thr[:], in_=pv[:, 4:8], func=ACT.Exp)
+
+        def dec_transposes(cb):
             dt = psum.tile([P, 2, 4, P], BF16, name="dt", tag="st")
             for cc in range(2):
                 for t in range(4):
                     c0 = (2 * cb + cc) * D + P * t
                     nc.tensor.transpose(dt[:, cc, t, :], dw[:, c0 : c0 + P], ident_b[:])
             d_banks.append(dt)
-        encode(0, 0)
-        encode(0, 1)
+
+        def dec_out(cb, copy):
+            copy(out=dgv[:, 2 * cb : 2 * cb + 2, :, :], in_=d_banks[cb][:].rearrange("p c t j -> p c j t"))
+
+        def quantise_dec():
+            nc.vector.quantize_mx(out=dec_q[:].bitcast(FP8X4), scales=dec_s[:], in_=dg[:])
+
+        x_transposes(0, 0)
+        x_transposes(0, 1)
+        enc_transposes(0)
+        enc_transposes(1)
+        x_out(0, 0)
+        x_out(0, 1, nc.vector.tensor_copy)
+        vector_transpose()
+        enc_out(0)
+        enc_out(1)
+        x_transposes(1, 0)
+        x_transposes(1, 1)
+        centre(0)
+        quantise_x(0)
+        quantise_enc()
+        x_out(1, 0)
+        x_out(1, 1)
+        enc_b_out()
+        threshold()
+        dec_transposes(0)
+        dec_transposes(1)
         x_transposes(2, 0)
         x_transposes(2, 1)
-        dgv = dg[:].rearrange("p (c j t) -> p c j t", c=4, t=4)
+        encode(0, 0)
+        encode(0, 1)
+        dec_out(0, nc.vector.tensor_copy)
         centre(1)
-        nc.scalar.copy(out=dgv[:, 0:2, :, :], in_=d_banks[0][:].rearrange("p c t j -> p c j t"))
         quantise_x(1)
-        nc.scalar.copy(out=dgv[:, 2:4, :, :], in_=d_banks[1][:].rearrange("p c t j -> p c j t"))
+        dec_out(1, nc.scalar.copy)
+        quantise_dec()
         x_out(2, 0)
         x_out(2, 1)
-        x_transposes(3, 0)
         centre(2)
-        nc.vector.quantize_mx(out=dec_q[:].bitcast(FP8X4), scales=dec_s[:], in_=dg[:])
         quantise_x(2)
+        load(4)
+        h_out(0, 0)
+        h_out(0, 1)
+        encode(0, 2)
+        encode(0, 3)
+        h_out(0, 2)
+        h_out(0, 3)
+        encode(1, 0)
+        encode(1, 1)
+        load(5)
+        jump(0, 0)
+        x_transposes(3, 0)
+        jump(0, 1)
+        jump(0, 2)
+        jump(0, 3)
+        x_transposes(3, 1)
+        h_out(1, 0)
+        h_out(1, 1)
+        encode(1, 2)
+        regroup(0)
+        quantise_a(0)
+        x_out(3, 0)
+        encode(1, 3)
+        a_transposes(0, 0)
+        x_transposes(4, 0)
+        h_out(1, 2)
+        h_out(1, 3)
+        x_out(3, 1)
+        encode(2, 0)
+        decode(0, 0)
+        encode(2, 1)
+        load(6)
+        decode(0, 1)
+        jump(1, 0)
+        jump(1, 1)
+        a_transposes(0, 1)
+        jump(1, 2)
+        jump(1, 3)
+        x_transposes(4, 1)
+        s_out(0, 0)
+        h_out(2, 0)
+        h_out(2, 1)
+        residual(0, 0)
+        decode(0, 2)
+        residual(0, 1)
+        x_out(4, 0)
+        encode(2, 2)
+        s_out(0, 1)
+        regroup(1)
+        centre(3)
+        quantise_a(1)
+        decode(0, 3)
+        encode(2, 3)
+        a_transposes(1, 0)
+        x_transposes(5, 0)
+        square(0, 0)
+        a_transposes(1, 1)
+        h_out(2, 2)
+        h_out(2, 3)
+        residual(0, 2)
+        quantise_x(3)
+        square(0, 1)
+        residual(0, 3)
+        x_out(4, 1)
+        encode(3, 0)
+        decode(1, 0)
+        encode(3, 1)
+        decode(1, 1)
 
         def steady(q):
             square(q - 2, 2)
             square(q - 2, 3)
             for t in range(4):
                 jump(q, t)
-            if q >= 0:
-                x_transposes(q + 3, 1)
+            x_transposes(q + 3, 1)
             s_out(q - 1, 0)
             h_out(q + 1, 0)
             h_out(q + 1, 1)
@@ -307,26 +401,21 @@ def tile_sae_t_kernel(tc, x, enc_w, enc_b, dec_w, dec_b, log_threshold, out_0, o
             encode(q + 1, 2)
             s_out(q - 1, 1)
             regroup(q)
-            if q >= 1:
-                centre(q + 2)
+            centre(q + 2)
             quantise_a(q)
-            if q >= 0:
-                x_out(q + 3, 0)
+            x_out(q + 3, 0)
             encode(q + 1, 3)
             a_transposes(q, 0)
-            if q >= 0:
-                x_transposes(q + 4, 0)
+            x_transposes(q + 4, 0)
             square(q - 1, 0)
             a_transposes(q, 1)
             h_out(q + 1, 2)
             h_out(q + 1, 3)
             residual(q - 1, 2)
-            if q >= 1:
-                quantise_x(q + 2)
+            quantise_x(q + 2)
             residual(q - 1, 3)
             square(q - 1, 1)
-            if q >= 0:
-                x_out(q + 3, 1)
+            x_out(q + 3, 1)
             encode(q + 2, 0)
             decode(q, 0)
             encode(q + 2, 1)
@@ -354,9 +443,8 @@ def tile_sae_t_kernel(tc, x, enc_w, enc_b, dec_w, dec_b, log_threshold, out_0, o
             residual(q - 1, 3)
             square(q - 1, 1)
 
-        for q in range(-1, ROUNDS + 2):
-            if q + 5 >= 4:
-                load(q + 5)
+        for q in range(2, ROUNDS + 2):
+            load(q + 5)
             if q < ROUNDS - 1:
                 steady(q)
             else:

@@ -180,10 +180,20 @@ def tile_sae_t_kernel(tc, x, enc_w, enc_b, dec_w, dec_b, log_threshold, out_0, o
         def regroup(q):
             if live(q):
                 ag_t[q] = work.tile([P, 4 * TOK], BF16, name="ag", tag="ag", bufs=2, align_bytes=64)
-                nc.vector.tensor_copy(
-                    out=ag_t[q][:].rearrange("p (c i t) -> p c t i", i=4, t=4),
-                    in_=ap_t[q][:].rearrange("p (t c i) -> p c t i", t=4, i=4),
-                )
+                if q == ROUNDS - 1:
+                    nc.vector.tensor_copy(
+                        out=ag_t[q][:].rearrange("p (c i t) -> p c t i", i=4, t=4),
+                        in_=ap_t[q][:].rearrange("p (t c i) -> p c t i", t=4, i=4),
+                    )
+                else:
+                    nc.gpsimd.tensor_scalar(
+                        out=ag_t[q][:].rearrange("p (c t) -> p c t", t=4),
+                        in0=ap_t[q][:].rearrange("p (t c) -> p c t", t=4),
+                        scalar1=1.0,
+                        scalar2=0.0,
+                        op0=ALU.mult,
+                        op1=ALU.add,
+                    )
 
         def quantise_a(q):
             if live(q):
@@ -314,8 +324,6 @@ def tile_sae_t_kernel(tc, x, enc_w, enc_b, dec_w, dec_b, log_threshold, out_0, o
         quantise_dec()
         x_out(2, 0)
         x_out(2, 1)
-        centre(2)
-        quantise_x(2)
         load(4)
         h_out(0, 0)
         h_out(0, 1)
@@ -325,130 +333,46 @@ def tile_sae_t_kernel(tc, x, enc_w, enc_b, dec_w, dec_b, log_threshold, out_0, o
         h_out(0, 3)
         encode(1, 0)
         encode(1, 1)
-        load(5)
-        jump(0, 0)
-        x_transposes(3, 0)
-        jump(0, 1)
-        jump(0, 2)
-        jump(0, 3)
-        x_transposes(3, 1)
-        h_out(1, 0)
-        h_out(1, 1)
-        encode(1, 2)
-        regroup(0)
-        quantise_a(0)
-        x_out(3, 0)
-        encode(1, 3)
-        a_transposes(0, 0)
-        x_transposes(4, 0)
-        h_out(1, 2)
-        h_out(1, 3)
-        x_out(3, 1)
-        encode(2, 0)
-        decode(0, 0)
-        encode(2, 1)
-        load(6)
-        decode(0, 1)
-        jump(1, 0)
-        jump(1, 1)
-        a_transposes(0, 1)
-        jump(1, 2)
-        jump(1, 3)
-        x_transposes(4, 1)
-        s_out(0, 0)
-        h_out(2, 0)
-        h_out(2, 1)
-        residual(0, 0)
-        decode(0, 2)
-        residual(0, 1)
-        x_out(4, 0)
-        encode(2, 2)
-        s_out(0, 1)
-        regroup(1)
-        centre(3)
-        quantise_a(1)
-        decode(0, 3)
-        encode(2, 3)
-        a_transposes(1, 0)
-        x_transposes(5, 0)
-        square(0, 0)
-        a_transposes(1, 1)
-        h_out(2, 2)
-        h_out(2, 3)
-        residual(0, 2)
-        quantise_x(3)
-        square(0, 1)
-        residual(0, 3)
-        x_out(4, 1)
-        encode(3, 0)
-        decode(1, 0)
-        encode(3, 1)
-        decode(1, 1)
 
-        def steady(q):
-            square(q - 2, 2)
-            square(q - 2, 3)
-            for t in range(4):
-                jump(q, t)
+        def round_steps(q):
+            x_transposes(q + 3, 0)
+            x_out(q + 3, 0)
             x_transposes(q + 3, 1)
-            s_out(q - 1, 0)
             h_out(q + 1, 0)
             h_out(q + 1, 1)
-            residual(q - 1, 0)
-            decode(q - 1, 2)
-            residual(q - 1, 1)
-            decode(q - 1, 3)
             encode(q + 1, 2)
-            s_out(q - 1, 1)
-            regroup(q)
-            centre(q + 2)
-            quantise_a(q)
-            x_out(q + 3, 0)
             encode(q + 1, 3)
-            a_transposes(q, 0)
-            x_transposes(q + 4, 0)
-            square(q - 1, 0)
-            a_transposes(q, 1)
-            h_out(q + 1, 2)
-            h_out(q + 1, 3)
-            residual(q - 1, 2)
-            quantise_x(q + 2)
-            residual(q - 1, 3)
-            square(q - 1, 1)
-            x_out(q + 3, 1)
-            encode(q + 2, 0)
-            decode(q, 0)
-            encode(q + 2, 1)
-            decode(q, 1)
-
-        def drain(q):
-            square(q - 2, 2)
-            square(q - 2, 3)
             for t in range(4):
                 jump(q, t)
-            residual(q - 1, 0)
-            s_out(q - 1, 0)
+            h_out(q + 1, 2)
+            h_out(q + 1, 3)
             regroup(q)
-            decode(q - 1, 2)
+            a_transposes(q, 0)
+            s_out(q, 0)
+            residual(q - 1, 0)
             residual(q - 1, 1)
-            quantise_a(q)
-            s_out(q - 1, 1)
+            decode(q - 1, 2)
             decode(q - 1, 3)
             square(q - 1, 0)
-            a_transposes(q, 0)
-            decode(q, 0)
-            decode(q, 1)
+            square(q - 1, 1)
             a_transposes(q, 1)
             residual(q - 1, 2)
             residual(q - 1, 3)
-            square(q - 1, 1)
+            s_out(q, 1)
+            x_out(q + 3, 1, nc.vector.tensor_copy)
+            square(q - 1, 2)
+            square(q - 1, 3)
+            centre(q + 2)
+            quantise_a(q)
+            quantise_x(q + 2)
+            decode(q, 0)
+            decode(q, 1)
+            encode(q + 2, 0)
+            encode(q + 2, 1)
 
-        for q in range(2, ROUNDS + 2):
+        for q in range(ROUNDS + 1):
             load(q + 5)
-            if q < ROUNDS - 1:
-                steady(q)
-            else:
-                drain(q)
+            round_steps(q)
 
         pl = psum.tile([P, 4 * ROUNDS], F32, name="pl", tag="r")
         nc.tensor.matmul(pl[:], lhsT=ones[:], rhs=lacc[:], start=True, stop=True)

@@ -104,15 +104,15 @@ def tile_sae_t_kernel(tc, x, enc_w, enc_b, dec_w, dec_b, log_threshold, out_0, o
             for jj in range(2):
                 for u in range(2):
                     c0 = (2 * b + jj) * 256 + P * u
-                    nc.tensor.transpose(bank[:, jj, u, :], srcw[:, c0 : c0 + P], ident_f[:])
+                    nc.tensor.transpose(bank[:, u, P * jj : P * jj + P], srcw[:, c0 : c0 + P], ident_f[:])
 
         def words_out(copy, bank, dst, b):
-            dstw = dst[:].bitcast(F32).rearrange("p (j r u) -> p j r u", j=4, u=2)
-            copy(out=dstw[:, 2 * b : 2 * b + 2, :, :], in_=bank[:].rearrange("p j u r -> p j r u"))
+            dstw = dst[:].bitcast(F32).rearrange("p (c u) -> p c u", u=2)
+            copy(out=dstw[:, 2 * P * b : 2 * P * (b + 1), :], in_=bank[:].rearrange("p u c -> p c u"))
 
         def x_transposes(q, b):
             if live(q):
-                xt_t[q, b] = psum.tile([P, 2, 2, P], F32, name="xt", tag="xt")
+                xt_t[q, b] = psum.tile([P, 2, 2 * P], F32, name="xt", tag="xt")
                 word_transposes(xs_t[q], b, xt_t[q, b])
 
         def x_out(q, b, copy=nc.scalar.copy):
@@ -121,13 +121,14 @@ def tile_sae_t_kernel(tc, x, enc_w, enc_b, dec_w, dec_b, log_threshold, out_0, o
                     xg_t[q] = work.tile([P, 4 * TOK], BF16, name="xg", tag="xg", bufs=6, align_bytes=64)
                 words_out(copy, xt_t[q, b], xg_t[q], b)
 
-        def centre(q):
+        def centre(q, b):
             if live(q):
-                xc_t[q] = work.tile([P, 4 * TOK], BF16, name="xc", tag="xc", bufs=2, align_bytes=64)
+                if q not in xc_t:
+                    xc_t[q] = work.tile([P, 4 * TOK], BF16, name="xc", tag="xc", bufs=2, align_bytes=64)
                 nc.vector.tensor_tensor(
-                    out=xc_t[q][:].rearrange("p (c t) -> p c t", t=4),
-                    in0=xg_t[q][:].rearrange("p (c t) -> p c t", t=4),
-                    in1=decb4.unsqueeze(1).to_broadcast([P, TOK, 4]),
+                    out=xc_t[q][:, 8 * P * b : 8 * P * (b + 1)].rearrange("p (c u e) -> p c u e", u=2, e=2),
+                    in0=xt_t[q, b][:].bitcast(BF16).rearrange("p u (c e) -> p c u e", e=2),
+                    in1=decb4.rearrange("p (u e) -> p u e", e=2).unsqueeze(1).to_broadcast([P, 2 * P, 2, 2]),
                     op=ALU.subtract,
                 )
 
@@ -180,7 +181,7 @@ def tile_sae_t_kernel(tc, x, enc_w, enc_b, dec_w, dec_b, log_threshold, out_0, o
         def regroup(q):
             if live(q):
                 ag_t[q] = work.tile([P, 4 * TOK], BF16, name="ag", tag="ag", bufs=2, align_bytes=64)
-                if q == ROUNDS - 1:
+                if q == 0 or q == ROUNDS - 1:
                     nc.vector.tensor_copy(
                         out=ag_t[q][:].rearrange("p (c i t) -> p c t i", i=4, t=4),
                         in_=ap_t[q][:].rearrange("p (t c i) -> p c t i", t=4, i=4),
@@ -227,7 +228,7 @@ def tile_sae_t_kernel(tc, x, enc_w, enc_b, dec_w, dec_b, log_threshold, out_0, o
 
         def decode(q, c):
             if live(q):
-                spare = q >= ROUNDS - 3 and c >= 2
+                spare = q >= ROUNDS - 2 and c >= 2
                 r_t[q, c] = psum.tile([P, TOK], F32, name="rps", tag="xt" if spare else "r")
                 mx(r_t[q, c], dec_q, dec_s, c, aq_t[q])
 
@@ -260,7 +261,7 @@ def tile_sae_t_kernel(tc, x, enc_w, enc_b, dec_w, dec_b, log_threshold, out_0, o
         dgv = dg[:].rearrange("p (c j t) -> p c j t", c=4, t=4)
 
         def enc_transposes(b):
-            et = psum.tile([P, 2, 2, P], F32, name="et", tag="h")
+            et = psum.tile([P, 2, 2 * P], F32, name="et", tag="h")
             word_transposes(ew, b, et)
             e_banks.append(et)
 
@@ -298,71 +299,73 @@ def tile_sae_t_kernel(tc, x, enc_w, enc_b, dec_w, dec_b, log_threshold, out_0, o
         enc_transposes(0)
         enc_transposes(1)
         x_out(0, 0)
-        x_out(0, 1, nc.vector.tensor_copy)
-        vector_transpose()
+        centre(0, 1)
+        centre(0, 0)
         enc_out(0)
         enc_out(1)
+        x_out(0, 1)
         x_transposes(1, 0)
         x_transposes(1, 1)
-        centre(0)
+        vector_transpose()
         quantise_x(0)
+        centre(1, 0)
         quantise_enc()
-        x_out(1, 0)
-        x_out(1, 1)
         enc_b_out()
+        centre(1, 1)
+        x_out(1, 0)
         threshold()
-        dec_transposes(0)
-        dec_transposes(1)
-        x_transposes(2, 0)
-        x_transposes(2, 1)
         encode(0, 0)
         encode(0, 1)
-        dec_out(0, nc.vector.tensor_copy)
-        centre(1)
+        dec_transposes(0)
+        dec_transposes(1)
         quantise_x(1)
-        dec_out(1, nc.scalar.copy)
-        quantise_dec()
-        x_out(2, 0)
-        x_out(2, 1)
-        load(4)
+        x_out(1, 1, nc.vector.tensor_copy)
         h_out(0, 0)
         h_out(0, 1)
         encode(0, 2)
         encode(0, 3)
+        dec_out(0, nc.scalar.copy)
+        dec_out(1, nc.scalar.copy)
+        load(4)
         h_out(0, 2)
         h_out(0, 3)
         encode(1, 0)
         encode(1, 1)
 
         def round_steps(q):
-            x_transposes(q + 3, 0)
-            x_out(q + 3, 0)
-            x_transposes(q + 3, 1)
+            x_transposes(q + 2, 0)
+            x_transposes(q + 2, 1)
             h_out(q + 1, 0)
             h_out(q + 1, 1)
+            x_out(q + 2, 0)
+            jump(q, 0)
+            jump(q, 1)
+            if q == 0:
+                quantise_dec()
+            jump(q, 2)
+            jump(q, 3)
+            regroup(q)
             encode(q + 1, 2)
             encode(q + 1, 3)
-            for t in range(4):
-                jump(q, t)
             h_out(q + 1, 2)
             h_out(q + 1, 3)
-            regroup(q)
             a_transposes(q, 0)
-            s_out(q, 0)
             residual(q - 1, 0)
             residual(q - 1, 1)
-            decode(q - 1, 2)
-            decode(q - 1, 3)
             square(q - 1, 0)
             square(q - 1, 1)
+            x_out(q + 2, 1, nc.vector.tensor_copy)
+            centre(q + 2, 0)
+            decode(q - 1, 2)
+            decode(q - 1, 3)
             a_transposes(q, 1)
+            s_out(q, 0)
             residual(q - 1, 2)
             residual(q - 1, 3)
+            centre(q + 2, 1)
             s_out(q, 1)
-            x_out(q + 3, 1, nc.vector.tensor_copy)
             square(q - 1, 2)
             square(q - 1, 3)
-            centre(q + 2)
             quantise_a(q)
             quantise_x(q + 2)
             decode(q, 0)

@@ -36,7 +36,7 @@ def tile_sae_t_kernel(tc, x, enc_w, enc_b, dec_w, dec_b, log_threshold, out_0, o
         psum = ctx.enter_context(tc.psum_pool(name="psum", bufs=2))
         ctx.enter_context(tc.manual_schedule())
 
-        xs_t, xt_t, xg_t, xc_t, xq_t, h_t, hf_t = {}, {}, {}, {}, {}, {}, {}
+        xs_t, xt_t, xc_t, xq_t, h_t, hf_t = {}, {}, {}, {}, {}, {}
         ap_t, ag_t, aq_t, st_t, ss_t, r_t, d_t = {}, {}, {}, {}, {}, {}, {}
 
         def live(q):
@@ -44,10 +44,12 @@ def tile_sae_t_kernel(tc, x, enc_w, enc_b, dec_w, dec_b, log_threshold, out_0, o
 
         def load(q):
             if live(q):
-                xs_t[q] = work.tile([P, 4 * D], BF16, name="xs", tag="xs", bufs=4)
-                nc.sync.dma_start(
-                    out=xs_t[q][:], in_=x[q * TOK : (q + 1) * TOK, :].rearrange("(p j) k -> p (j k)", j=4)
-                )
+                xs_t[q] = work.tile([P, 4 * D], BF16, name="xs", tag="xs", bufs=6)
+                rows = x[q * TOK : (q + 1) * TOK, :].rearrange("(p j) k -> p (j k)", j=4)
+                pieces = 2 if q == 0 else 1
+                for i in range(pieces):
+                    cols = slice(i * 4 * D // pieces, (i + 1) * 4 * D // pieces)
+                    nc.sync.dma_start(out=xs_t[q][:, cols], in_=rows[:, cols])
 
         warm = consts.tile([P, 1], F32, name="warm")
         nc.vector.memset(warm[:], 0.0)
@@ -65,6 +67,9 @@ def tile_sae_t_kernel(tc, x, enc_w, enc_b, dec_w, dec_b, log_threshold, out_0, o
         make_identity(nc, ident_b[:])
 
         nc.sync.dma_start(out=vw[0:2, :], in_=dec_b.rearrange("(u w) -> u w", u=2))
+        nc.scalar.dma_start(out=vb[0:4, :], in_=enc_b.rearrange("(t p) -> t p", p=P))
+        nc.scalar.dma_start(out=vb[4:8, :], in_=log_threshold.rearrange("(t p) -> t p", p=P))
+        nc.scalar.dma_start(out=vb[8:12, :], in_=dec_b.rearrange("(t p) -> t p", p=P))
         load(0)
         ew = consts.tile([P, 4 * D], BF16, name="ew")
         nc.sync.dma_start(
@@ -72,12 +77,10 @@ def tile_sae_t_kernel(tc, x, enc_w, enc_b, dec_w, dec_b, log_threshold, out_0, o
             in_=enc_w.rearrange("(t r) k -> r t k", r=P),
         )
         load(1)
-        nc.sync.dma_start(out=vb[0:4, :], in_=enc_b.rearrange("(t p) -> t p", p=P))
-        nc.sync.dma_start(out=vb[4:8, :], in_=log_threshold.rearrange("(t p) -> t p", p=P))
         dw = consts.tile([P, 4 * D], BF16, name="dw")
         nc.sync.dma_start(
-            out=dw[:].rearrange("j (u eh) -> j u eh", u=2),
-            in_=dec_w.rearrange("(u j e) h -> j u (e h)", u=2, e=2),
+            out=dw[:].rearrange("r (c h) -> r c h", c=4),
+            in_=dec_w.rearrange("(c r) h -> r c h", r=P),
         )
         load(2)
         load(3)
@@ -88,8 +91,10 @@ def tile_sae_t_kernel(tc, x, enc_w, enc_b, dec_w, dec_b, log_threshold, out_0, o
         nc.vector.tensor_copy(out=decw2[:], in_=pw[:, 0:2])
         decb4 = decw2[:].bitcast(BF16)
         decbf = consts.tile([P, 4], F32, name="decbf")
-        nc.vector.tensor_copy(out=decbf[:], in_=decb4)
-        lacc = consts.tile([P, 4 * ROUNDS], F32, name="lacc")
+        ones_b = consts.tile([P, 2], BF16, name="ones_b")
+        nc.vector.memset(ones_b[:], 1.0)
+        btab = consts.tile([P, D], BF16, name="btab")
+        lacc = consts.tile([P, 2 * ROUNDS + 3], F32, name="lacc")
         encb = consts.tile([P, 4], F32, name="encb")
         thr = consts.tile([P, 4], F32, name="thr")
         enc_q = consts.tile([P, D], U32, name="enc_q", align_bytes=64)
@@ -112,14 +117,20 @@ def tile_sae_t_kernel(tc, x, enc_w, enc_b, dec_w, dec_b, log_threshold, out_0, o
 
         def x_transposes(q, b):
             if live(q):
-                xt_t[q, b] = psum.tile([P, 2, 2 * P], F32, name="xt", tag="xt")
+                xt_t[q, b] = psum.tile([P, 2, 2 * P], F32, name="xt", tag="x_sum" if q < 2 and b == 1 else "xt", bufs=1)
                 word_transposes(xs_t[q], b, xt_t[q, b])
 
-        def x_out(q, b, copy=nc.scalar.copy):
+        def x_sums(q):
             if live(q):
-                if b == 0:
-                    xg_t[q] = work.tile([P, 4 * TOK], BF16, name="xg", tag="xg", bufs=6, align_bytes=64)
-                words_out(copy, xt_t[q, b], xg_t[q], b)
+                for i in range(4):
+                    for j in range(4):
+                        nc.tensor.matmul(
+                            x_sum[:, q, i, :],
+                            lhsT=xs_t[q][:, j * D + i * P : j * D + (i + 1) * P],
+                            rhs=ones_b[:],
+                            start=j == 0,
+                            stop=j == 3,
+                        )
 
         def centre(q, b):
             if live(q):
@@ -142,21 +153,21 @@ def tile_sae_t_kernel(tc, x, enc_w, enc_b, dec_w, dec_b, log_threshold, out_0, o
             if live(q):
                 xq_t[q] = quantise(xc_t[q], "x")
 
-        def mx(bank, w_q, w_s, i, moving):
+        def mx(bank, stationary, i, moving, start=True, stop=True):
             nc.tensor.matmul_mx(
                 out=bank[:],
-                lhsT=w_q[:, i * P : (i + 1) * P].bitcast(FP8X4),
-                lhsT_scale=w_s[:, i * P : (i + 1) * P],
+                lhsT=stationary[0][:, i * P : (i + 1) * P].bitcast(FP8X4),
+                lhsT_scale=stationary[1][:, i * P : (i + 1) * P],
                 rhs=moving[0][:].bitcast(FP8X4),
                 rhs_scale=moving[1][:],
-                start=True,
-                stop=True,
+                start=start,
+                stop=stop,
             )
 
         def encode(q, t):
             if live(q):
                 h_t[q, t] = psum.tile([P, TOK], F32, name="hps", tag="r" if q == 0 and t >= 2 else "h")
-                mx(h_t[q, t], enc_q, enc_s, t, xq_t[q])
+                mx(h_t[q, t], (enc_q, enc_s), t, xq_t[q])
 
         def h_out(q, t):
             if live(q):
@@ -202,7 +213,7 @@ def tile_sae_t_kernel(tc, x, enc_w, enc_b, dec_w, dec_b, log_threshold, out_0, o
 
         def a_transposes(q, b):
             if live(q):
-                st_t[q, b] = psum.tile([P, 2, D], BF16, name="st", tag="st")
+                st_t[q, b] = psum.tile([P, 2, D], BF16, name="st", tag="xt" if q == ROUNDS - 1 and b else "st", bufs=1)
                 for jj in range(2):
                     for t in range(4):
                         c0 = t * TOK + (2 * b + jj) * P
@@ -226,33 +237,36 @@ def tile_sae_t_kernel(tc, x, enc_w, enc_b, dec_w, dec_b, log_threshold, out_0, o
                         in_=ss_t[q][:],
                     )
 
-        def decode(q, c):
+        def decode(q, j):
             if live(q):
-                spare = q >= ROUNDS - 2 and c >= 2
-                r_t[q, c] = psum.tile([P, TOK], F32, name="rps", tag="xt" if spare else "r")
-                mx(r_t[q, c], dec_q, dec_s, c, aq_t[q])
+                r_t[q, j] = psum.tile([P, D], F32, name="rps", tag="h" if q >= ROUNDS - 2 and j >= 2 else "r")
+                mx(r_t[q, j], aq_t[q], j, (dec_q, dec_s))
 
-        def residual(q, c):
+        def add_up(q, j):
             if live(q):
-                d_t[q, c] = work.tile([P, TOK], F32, name="d0", tag="d0", bufs=8)
+                mx(r_sum, aq_t[q], j, (dec_q, dec_s), start=q + j == 0, stop=q == ROUNDS - 1 and j == 3)
+
+        def residual(q, j):
+            if live(q):
+                if j == 0:
+                    d_t[q] = work.tile([P, 4 * D], F32, name="d0", tag="d0", bufs=2)
                 nc.vector.scalar_tensor_tensor(
-                    out=d_t[q, c][:],
-                    in0=xg_t[q][:].rearrange("p (c t) -> p c t", t=4)[:, :, c],
+                    out=d_t[q][:, j * D : (j + 1) * D],
+                    in0=xs_t[q][:, j * D : (j + 1) * D],
                     scalar=-64.0,
-                    in1=r_t[q, c][:],
+                    in1=r_t[q, j][:],
                     op0=ALU.mult,
                     op1=ALU.add,
                 )
 
-        def square(q, c):
+        def square(q, half):
             if live(q):
+                d_half = d_t[q][:, 2 * half * D : 2 * (half + 1) * D]
                 nc.scalar.activation(
-                    out=d_t[q, c][:],
-                    in_=d_t[q, c][:],
+                    out=d_half,
+                    in_=d_half,
                     func=ACT.Square,
-                    bias=decbf[:, c : c + 1],
-                    scale=1.0,
-                    accum_out=lacc[:, 4 * q + c : 4 * q + c + 1],
+                    accum_out=lacc[:, 2 * q + half : 2 * q + half + 1],
                 )
 
         e_banks = []
@@ -276,12 +290,13 @@ def tile_sae_t_kernel(tc, x, enc_w, enc_b, dec_w, dec_b, log_threshold, out_0, o
 
         def enc_b_out():
             nc.vector.tensor_copy(out=encb[:], in_=pv[:, 0:4])
+            nc.vector.tensor_copy(out=decbf[:], in_=pv[:, 8:12])
 
         def threshold():
             nc.scalar.activation(out=thr[:], in_=pv[:, 4:8], func=ACT.Exp)
 
         def dec_transposes(cb):
-            dt = psum.tile([P, 2, 4, P], BF16, name="dt", tag="st")
+            dt = psum.tile([P, 2, 4, P], BF16, name="dt", tag="r_sum" if cb else "st", bufs=1)
             for cc in range(2):
                 for t in range(4):
                     c0 = (2 * cb + cc) * D + P * t
@@ -294,90 +309,123 @@ def tile_sae_t_kernel(tc, x, enc_w, enc_b, dec_w, dec_b, log_threshold, out_0, o
         def quantise_dec():
             nc.vector.quantize_mx(out=dec_q[:].bitcast(FP8X4), scales=dec_s[:], in_=dg[:])
 
+        vector_transpose()
+        enc_b_out()
+        threshold()
         x_transposes(0, 0)
         x_transposes(0, 1)
+        centre(0, 0)
+        centre(0, 1)
         enc_transposes(0)
         enc_transposes(1)
-        x_out(0, 0)
-        centre(0, 1)
-        centre(0, 0)
         enc_out(0)
         enc_out(1)
-        x_out(0, 1)
         x_transposes(1, 0)
-        x_transposes(1, 1)
-        vector_transpose()
         quantise_x(0)
-        centre(1, 0)
         quantise_enc()
-        enc_b_out()
+        centre(1, 0)
+        x_transposes(1, 1)
         centre(1, 1)
-        x_out(1, 0)
-        threshold()
+        dec_transposes(0)
         encode(0, 0)
         encode(0, 1)
-        dec_transposes(0)
-        dec_transposes(1)
-        quantise_x(1)
-        x_out(1, 1, nc.vector.tensor_copy)
         h_out(0, 0)
         h_out(0, 1)
         encode(0, 2)
         encode(0, 3)
-        dec_out(0, nc.scalar.copy)
-        dec_out(1, nc.scalar.copy)
-        load(4)
+        dec_transposes(1)
+        quantise_x(1)
         h_out(0, 2)
         h_out(0, 3)
+        load(4)
         encode(1, 0)
         encode(1, 1)
+        dec_out(0, nc.scalar.copy)
+        dec_out(1, nc.scalar.copy)
+
+        r_sum = psum.tile([P, D], F32, name="r_sum", tag="r_sum", bufs=1)
+        x_sum = psum.tile([P, ROUNDS, 4, 2], F32, name="x_sum", tag="x_sum", bufs=1)
 
         def round_steps(q):
             x_transposes(q + 2, 0)
-            x_transposes(q + 2, 1)
             h_out(q + 1, 0)
             h_out(q + 1, 1)
-            x_out(q + 2, 0)
+            square(q - 2, 1)
             jump(q, 0)
             jump(q, 1)
-            if q == 0:
-                quantise_dec()
             jump(q, 2)
             jump(q, 3)
-            regroup(q)
+            add_up(q - 1, 0)
             encode(q + 1, 2)
             encode(q + 1, 3)
             h_out(q + 1, 2)
             h_out(q + 1, 3)
-            a_transposes(q, 0)
-            residual(q - 1, 0)
-            residual(q - 1, 1)
-            square(q - 1, 0)
-            square(q - 1, 1)
-            x_out(q + 2, 1, nc.vector.tensor_copy)
             centre(q + 2, 0)
+            a_transposes(q, 0)
+            x_transposes(q + 2, 1)
+            residual(q - 1, 0)
+            regroup(q)
+            residual(q - 1, 1)
+            s_out(q, 0)
+            square(q - 1, 0)
             decode(q - 1, 2)
             decode(q - 1, 3)
+            centre(q + 2, 1)
+            x_sums(q)
             a_transposes(q, 1)
-            s_out(q, 0)
             residual(q - 1, 2)
             residual(q - 1, 3)
-            centre(q + 2, 1)
             s_out(q, 1)
-            square(q - 1, 2)
-            square(q - 1, 3)
-            quantise_a(q)
+            add_up(q - 1, 1)
+            add_up(q - 1, 2)
+            add_up(q - 1, 3)
             quantise_x(q + 2)
-            decode(q, 0)
-            decode(q, 1)
+            if q == 0: quantise_dec()
+            quantise_a(q)
             encode(q + 2, 0)
             encode(q + 2, 1)
+            decode(q, 0)
+            decode(q, 1)
 
         for q in range(ROUNDS + 1):
             load(q + 5)
+            if q == 3:
+                nc.sync.dma_start(out=btab[:], in_=dec_b.partition_broadcast(P))
             round_steps(q)
+        square(ROUNDS - 1, 1)
 
-        pl = psum.tile([P, 4 * ROUNDS], F32, name="pl", tag="r")
+        junk = consts.tile([P, D], F32, name="junk")
+        nc.vector.scalar_tensor_tensor(
+            out=junk[:, 0 : 4 * ROUNDS].rearrange("p (q i) -> p q i", i=4),
+            in0=x_sum[:, :, :, 0],
+            scalar=-128.0,
+            in1=decbf[:].unsqueeze(1).to_broadcast([P, ROUNDS, 4]),
+            op0=ALU.mult,
+            op1=ALU.mult,
+            accum_out=lacc[:, 2 * ROUNDS : 2 * ROUNDS + 1],
+        )
+        junk2 = consts.tile([P, 4], F32, name="junk2")
+        nc.vector.scalar_tensor_tensor(
+            out=junk2[:],
+            in0=decbf[:],
+            scalar=float(N_TOK),
+            in1=decbf[:],
+            op0=ALU.mult,
+            op1=ALU.mult,
+            accum_out=lacc[:, 2 * ROUNDS + 1 : 2 * ROUNDS + 2],
+        )
+        junk3 = consts.tile([P, D], F32, name="junk3")
+        nc.vector.scalar_tensor_tensor(
+            out=junk3[:],
+            in0=r_sum[:],
+            scalar=2.0,
+            in1=btab[:],
+            op0=ALU.mult,
+            op1=ALU.mult,
+            accum_out=lacc[:, 2 * ROUNDS + 2 : 2 * ROUNDS + 3],
+        )
+
+        pl = psum.tile([P, 2 * ROUNDS + 3], F32, name="pl", tag="r")
         nc.tensor.matmul(pl[:], lhsT=ones[:], rhs=lacc[:], start=True, stop=True)
         tot = consts.tile([P, 1], F32, name="tot")
         nc.vector.tensor_reduce(out=tot[:], in_=pl[:], axis=AX.X, op=ALU.add)

@@ -44,7 +44,7 @@ def tile_sae_t_kernel(tc, x, enc_w, enc_b, dec_w, dec_b, log_threshold, out_0, o
 
         def load(q):
             if live(q):
-                xs_t[q] = work.tile([P, 4 * D], BF16, name="xs", tag="xs", bufs=6)
+                xs_t[q] = work.tile([P, 4 * D], BF16, name="xs", tag="xs", bufs=7)
                 rows = x[q * TOK : (q + 1) * TOK, :].rearrange("(p j) k -> p (j k)", j=4)
                 pieces = 2 if q == 0 else 1
                 for i in range(pieces):
@@ -77,13 +77,14 @@ def tile_sae_t_kernel(tc, x, enc_w, enc_b, dec_w, dec_b, log_threshold, out_0, o
             in_=enc_w.rearrange("(t r) k -> r t k", r=P),
         )
         load(1)
+        load(2)
         dw = consts.tile([P, 4 * D], BF16, name="dw")
         nc.sync.dma_start(
             out=dw[:].rearrange("r (c h) -> r c h", c=4),
             in_=dec_w.rearrange("(c r) h -> r c h", r=P),
         )
-        load(2)
         load(3)
+        load(4)
 
         pw = psum.tile([P, P], F32, name="pw", tag="r")
         nc.tensor.transpose(pw[:], vw[:].bitcast(F32), ident_f[:])
@@ -94,7 +95,7 @@ def tile_sae_t_kernel(tc, x, enc_w, enc_b, dec_w, dec_b, log_threshold, out_0, o
         ones_b = consts.tile([P, 2], BF16, name="ones_b")
         nc.vector.memset(ones_b[:], 1.0)
         btab = consts.tile([P, D], BF16, name="btab")
-        lacc = consts.tile([P, 2 * ROUNDS + 3], F32, name="lacc")
+        lacc = consts.tile([P, 2 * ROUNDS + 5], F32, name="lacc")
         encb = consts.tile([P, 4], F32, name="encb")
         thr = consts.tile([P, 4], F32, name="thr")
         enc_q = consts.tile([P, D], U32, name="enc_q", align_bytes=64)
@@ -117,7 +118,7 @@ def tile_sae_t_kernel(tc, x, enc_w, enc_b, dec_w, dec_b, log_threshold, out_0, o
 
         def x_transposes(q, b):
             if live(q):
-                xt_t[q, b] = psum.tile([P, 2, 2 * P], F32, name="xt", tag="x_sum" if q < 2 and b == 1 else "xt", bufs=1)
+                xt_t[q, b] = psum.tile([P, 2, 2 * P], F32, name="xt", tag="x_sum" if q < 3 and b == 1 else "xt", bufs=1)
                 word_transposes(xs_t[q], b, xt_t[q, b])
 
         def x_sums(q):
@@ -144,8 +145,8 @@ def tile_sae_t_kernel(tc, x, enc_w, enc_b, dec_w, dec_b, log_threshold, out_0, o
                 )
 
         def quantise(src, tag):
-            codes = work.tile([P, TOK], U32, name=tag + "_codes", tag=tag + "_codes", bufs=3, align_bytes=64)
-            scales = work.tile([P, TOK], U8, name=tag + "_scales", tag=tag + "_scales", bufs=3, align_bytes=64)
+            codes = work.tile([P, TOK], U32, name=tag + "_codes", tag=tag + "_codes", bufs=4, align_bytes=64)
+            scales = work.tile([P, TOK], U8, name=tag + "_scales", tag=tag + "_scales", bufs=4, align_bytes=64)
             nc.vector.quantize_mx(out=codes[:].bitcast(FP8X4), scales=scales[:], in_=src[:])
             return codes, scales
 
@@ -192,7 +193,7 @@ def tile_sae_t_kernel(tc, x, enc_w, enc_b, dec_w, dec_b, log_threshold, out_0, o
         def regroup(q):
             if live(q):
                 ag_t[q] = work.tile([P, 4 * TOK], BF16, name="ag", tag="ag", bufs=2, align_bytes=64)
-                if q == 0 or q == ROUNDS - 1:
+                if q == 0 or q >= ROUNDS - 3:
                     nc.vector.tensor_copy(
                         out=ag_t[q][:].rearrange("p (c i t) -> p c t i", i=4, t=4),
                         in_=ap_t[q][:].rearrange("p (t c i) -> p c t i", t=4, i=4),
@@ -227,19 +228,16 @@ def tile_sae_t_kernel(tc, x, enc_w, enc_b, dec_w, dec_b, log_threshold, out_0, o
                     ss_t[q] = work.tile([P, 4 * D], F32, name="ssb", tag="ssb", bufs=3)
                 s_half = ss_t[q][:, 2 * b * D : (2 * b + 2) * D]
                 a_half = st_t[q, b][:].rearrange("p j h -> p (j h)")
-                if q == ROUNDS - 1 and b == 1:
-                    nc.vector.tensor_single_scalar(out=s_half, in_=a_half, scalar=0.0, op=ALU.is_gt)
-                else:
-                    nc.scalar.activation(out=s_half, in_=a_half, func=ACT.Sign)
-                if b == 1:
-                    nc.sync.dma_start(
-                        out=out_0[q * TOK : (q + 1) * TOK, :].rearrange("(p j) h -> p (j h)", j=4),
-                        in_=ss_t[q][:],
-                    )
+                nc.scalar.activation(out=s_half, in_=a_half, func=ACT.Sign)
+                rows = out_0[q * TOK : (q + 1) * TOK, :].rearrange("(p j) h -> p (j h)", j=4)
+                if q == ROUNDS - 1:
+                    nc.sync.dma_start(out=rows[:, 2 * b * D : (2 * b + 2) * D], in_=s_half)
+                elif b == 1:
+                    nc.sync.dma_start(out=rows, in_=ss_t[q][:])
 
         def decode(q, j):
             if live(q):
-                r_t[q, j] = psum.tile([P, D], F32, name="rps", tag="h" if q >= ROUNDS - 2 and j >= 2 else "r")
+                r_t[q, j] = psum.tile([P, D], F32, name="rps", tag="h" if q >= ROUNDS - 2 and j >= 2 else "xt" if q >= ROUNDS - 4 and j == 2 else "r", bufs=1 if ROUNDS - 4 <= q < ROUNDS - 2 and j == 2 else 2)
                 mx(r_t[q, j], aq_t[q], j, (dec_q, dec_s))
 
         def add_up(q, j):
@@ -261,13 +259,11 @@ def tile_sae_t_kernel(tc, x, enc_w, enc_b, dec_w, dec_b, log_threshold, out_0, o
 
         def square(q, half):
             if live(q):
-                d_half = d_t[q][:, 2 * half * D : 2 * (half + 1) * D]
-                nc.scalar.activation(
-                    out=d_half,
-                    in_=d_half,
-                    func=ACT.Square,
-                    accum_out=lacc[:, 2 * q + half : 2 * q + half + 1],
-                )
+                square_columns(q, 2 * half, 2, 2 * q + half)
+
+        def square_columns(q, j, n, column):
+            d = d_t[q][:, j * D : (j + n) * D]
+            nc.scalar.activation(out=d, in_=d, func=ACT.Square, accum_out=lacc[:, column : column + 1])
 
         e_banks = []
         d_banks = []
@@ -311,6 +307,16 @@ def tile_sae_t_kernel(tc, x, enc_w, enc_b, dec_w, dec_b, log_threshold, out_0, o
 
         vector_transpose()
         enc_b_out()
+        b_sq = consts.tile([P, 4], F32, name="b_sq")
+        nc.vector.scalar_tensor_tensor(
+            out=b_sq[:],
+            in0=decbf[:],
+            scalar=float(N_TOK),
+            in1=decbf[:],
+            op0=ALU.mult,
+            op1=ALU.mult,
+            accum_out=lacc[:, 2 * ROUNDS + 4 : 2 * ROUNDS + 5],
+        )
         threshold()
         x_transposes(0, 0)
         x_transposes(0, 1)
@@ -321,48 +327,81 @@ def tile_sae_t_kernel(tc, x, enc_w, enc_b, dec_w, dec_b, log_threshold, out_0, o
         enc_out(0)
         enc_out(1)
         x_transposes(1, 0)
-        quantise_x(0)
-        quantise_enc()
-        centre(1, 0)
         x_transposes(1, 1)
+        quantise_x(0)
+        centre(1, 0)
+        quantise_enc()
+        x_transposes(2, 0)
         centre(1, 1)
-        dec_transposes(0)
         encode(0, 0)
         encode(0, 1)
+        x_transposes(2, 1)
+        centre(2, 0)
         h_out(0, 0)
         h_out(0, 1)
+        quantise_x(1)
         encode(0, 2)
         encode(0, 3)
-        dec_transposes(1)
-        quantise_x(1)
+        centre(2, 1)
         h_out(0, 2)
         h_out(0, 3)
-        load(4)
         encode(1, 0)
         encode(1, 1)
-        dec_out(0, nc.scalar.copy)
-        dec_out(1, nc.scalar.copy)
+        dec_transposes(0)
+        dec_transposes(1)
+        x_transposes(3, 0)
 
         r_sum = psum.tile([P, D], F32, name="r_sum", tag="r_sum", bufs=1)
         x_sum = psum.tile([P, ROUNDS, 4, 2], F32, name="x_sum", tag="x_sum", bufs=1)
 
-        def round_steps(q):
-            x_transposes(q + 2, 0)
-            h_out(q + 1, 0)
+        def first_round():
+            h_out(1, 0)
+            h_out(1, 1)
+            encode(1, 2)
+            encode(1, 3)
+            jump(0, 0)
+            jump(0, 1)
+            quantise_x(2)
+            jump(0, 2)
+            jump(0, 3)
+            dec_out(0, nc.scalar.copy)
+            dec_out(1, nc.scalar.copy)
+            h_out(1, 2)
+            h_out(1, 3)
+            centre(3, 0)
+            a_transposes(0, 0)
+            x_transposes(3, 1)
+            regroup(0)
+            s_out(0, 0)
+            encode(2, 0)
+            encode(2, 1)
+            centre(3, 1)
+            x_sums(0)
+            a_transposes(0, 1)
+            x_transposes(4, 0)
+            h_out(2, 0)
+            s_out(0, 1)
+            quantise_dec()
+            quantise_x(3)
+            quantise_a(0)
+            decode(0, 0)
+            decode(0, 1)
+
+        def steady_round(q):
             h_out(q + 1, 1)
+            add_up(q - 1, 0)
+            encode(q + 1, 2)
+            encode(q + 1, 3)
             square(q - 2, 1)
             jump(q, 0)
             jump(q, 1)
             jump(q, 2)
             jump(q, 3)
-            add_up(q - 1, 0)
-            encode(q + 1, 2)
-            encode(q + 1, 3)
             h_out(q + 1, 2)
             h_out(q + 1, 3)
-            centre(q + 2, 0)
+            centre(q + 3, 0)
             a_transposes(q, 0)
-            x_transposes(q + 2, 1)
+            x_transposes(q + 3, 1)
             residual(q - 1, 0)
             regroup(q)
             residual(q - 1, 1)
@@ -370,29 +409,63 @@ def tile_sae_t_kernel(tc, x, enc_w, enc_b, dec_w, dec_b, log_threshold, out_0, o
             square(q - 1, 0)
             decode(q - 1, 2)
             decode(q - 1, 3)
-            centre(q + 2, 1)
+            centre(q + 3, 1)
+            encode(q + 2, 0)
+            encode(q + 2, 1)
             x_sums(q)
             a_transposes(q, 1)
+            x_transposes(q + 4, 0)
             residual(q - 1, 2)
             residual(q - 1, 3)
+            h_out(q + 2, 0)
             s_out(q, 1)
             add_up(q - 1, 1)
             add_up(q - 1, 2)
             add_up(q - 1, 3)
-            quantise_x(q + 2)
-            if q == 0: quantise_dec()
+            quantise_x(q + 3)
             quantise_a(q)
-            encode(q + 2, 0)
-            encode(q + 2, 1)
             decode(q, 0)
             decode(q, 1)
 
-        for q in range(ROUNDS + 1):
+        def last_round():
+            q = ROUNDS - 1
+            decode(q - 1, 2)
+            decode(q - 1, 3)
+            square(q - 2, 1)
+            for t in range(4):
+                jump(q, t)
+            a_transposes(q, 0)
+            a_transposes(q, 1)
+            residual(q - 1, 0)
+            regroup(q)
+            s_out(q, 0)
+            residual(q - 1, 1)
+            square(q - 1, 0)
+            quantise_a(q)
+            residual(q - 1, 2)
+            residual(q - 1, 3)
+            s_out(q, 1)
+            for j in range(4):
+                add_up(q - 1, j)
+            square(q - 1, 1)
+            x_sums(q)
+            for j in range(4):
+                decode(q, j)
+            for j in range(4):
+                add_up(q, j)
+            for j in range(3):
+                residual(q, j)
+                square_columns(q, j, 1, 2 * q + j)
+            residual(q, 3)
+
+        load(5)
+        first_round()
+        for q in range(1, ROUNDS - 1):
             load(q + 5)
             if q == 3:
                 nc.sync.dma_start(out=btab[:], in_=dec_b.partition_broadcast(P))
-            round_steps(q)
-        square(ROUNDS - 1, 1)
+            steady_round(q)
+        last_round()
 
         junk = consts.tile([P, D], F32, name="junk")
         nc.vector.scalar_tensor_tensor(
@@ -402,30 +475,30 @@ def tile_sae_t_kernel(tc, x, enc_w, enc_b, dec_w, dec_b, log_threshold, out_0, o
             in1=decbf[:].unsqueeze(1).to_broadcast([P, ROUNDS, 4]),
             op0=ALU.mult,
             op1=ALU.mult,
-            accum_out=lacc[:, 2 * ROUNDS : 2 * ROUNDS + 1],
+            accum_out=lacc[:, 2 * ROUNDS + 2 : 2 * ROUNDS + 3],
         )
-        junk2 = consts.tile([P, 4], F32, name="junk2")
+        junk2 = consts.tile([P, D], F32, name="junk2")
         nc.vector.scalar_tensor_tensor(
             out=junk2[:],
-            in0=decbf[:],
-            scalar=float(N_TOK),
-            in1=decbf[:],
-            op0=ALU.mult,
-            op1=ALU.mult,
-            accum_out=lacc[:, 2 * ROUNDS + 1 : 2 * ROUNDS + 2],
-        )
-        junk3 = consts.tile([P, D], F32, name="junk3")
-        nc.vector.scalar_tensor_tensor(
-            out=junk3[:],
             in0=r_sum[:],
             scalar=2.0,
             in1=btab[:],
             op0=ALU.mult,
             op1=ALU.mult,
-            accum_out=lacc[:, 2 * ROUNDS + 2 : 2 * ROUNDS + 3],
+            accum_out=lacc[:, 2 * ROUNDS + 3 : 2 * ROUNDS + 4],
+        )
+        d = d_t[ROUNDS - 1][:, 3 * D : 4 * D]
+        nc.vector.scalar_tensor_tensor(
+            out=junk[:],
+            in0=d,
+            scalar=1.0,
+            in1=d,
+            op0=ALU.mult,
+            op1=ALU.mult,
+            accum_out=lacc[:, 2 * ROUNDS + 1 : 2 * ROUNDS + 2],
         )
 
-        pl = psum.tile([P, 2 * ROUNDS + 3], F32, name="pl", tag="r")
+        pl = psum.tile([P, 2 * ROUNDS + 5], F32, name="pl", tag="r")
         nc.tensor.matmul(pl[:], lhsT=ones[:], rhs=lacc[:], start=True, stop=True)
         tot = consts.tile([P, 1], F32, name="tot")
         nc.vector.tensor_reduce(out=tot[:], in_=pl[:], axis=AX.X, op=ALU.add)

@@ -66,16 +66,17 @@ def tile_sae_t_kernel(tc, x, enc_w, enc_b, dec_w, dec_b, log_threshold, out_0, o
         ident_b = consts.tile([P, P], BF16, name="ident_b")
         make_identity(nc, ident_b[:])
 
-        nc.sync.dma_start(out=vw[0:2, :], in_=dec_b.rearrange("(u w) -> u w", u=2))
+        nc.scalar.dma_start(out=vw[0:2, :], in_=dec_b.rearrange("(u w) -> u w", u=2))
         nc.scalar.dma_start(out=vb[0:4, :], in_=enc_b.rearrange("(t p) -> t p", p=P))
         nc.scalar.dma_start(out=vb[4:8, :], in_=log_threshold.rearrange("(t p) -> t p", p=P))
         nc.scalar.dma_start(out=vb[8:12, :], in_=dec_b.rearrange("(t p) -> t p", p=P))
         load(0)
         ew = consts.tile([P, 4 * D], BF16, name="ew")
-        nc.sync.dma_start(
-            out=ew[:].rearrange("r (t k) -> r t k", t=4),
-            in_=enc_w.rearrange("(t r) k -> r t k", r=P),
-        )
+        for b in range(2):
+            nc.sync.dma_start(
+                out=ew[:, 2 * b * D : 2 * (b + 1) * D].rearrange("r (t k) -> r t k", t=2),
+                in_=enc_w[2 * b * P : 2 * (b + 1) * P, :].rearrange("(t r) k -> r t k", r=P),
+            )
         load(1)
         load(2)
         dw = consts.tile([P, 4 * D], BF16, name="dw")
@@ -194,10 +195,12 @@ def tile_sae_t_kernel(tc, x, enc_w, enc_b, dec_w, dec_b, log_threshold, out_0, o
             if live(q):
                 ag_t[q] = work.tile([P, 4 * TOK], BF16, name="ag", tag="ag", bufs=2, align_bytes=64)
                 if q == 0 or q >= ROUNDS - 3:
-                    nc.vector.tensor_copy(
-                        out=ag_t[q][:].rearrange("p (c i t) -> p c t i", i=4, t=4),
-                        in_=ap_t[q][:].rearrange("p (t c i) -> p c t i", t=4, i=4),
-                    )
+                    split = TOK // 32 if q == ROUNDS - 1 else 0
+                    grouped = ag_t[q][:].rearrange("p (c i t) -> p c t i", i=4, t=4)
+                    plain = ap_t[q][:].rearrange("p (t c i) -> p c t i", t=4, i=4)
+                    nc.vector.tensor_copy(out=grouped[:, split:, :, :], in_=plain[:, split:, :, :])
+                    if split:
+                        nc.scalar.copy(out=grouped[:, 0:split, :, :], in_=plain[:, 0:split, :, :])
                 else:
                     nc.gpsimd.tensor_scalar(
                         out=ag_t[q][:].rearrange("p (c t) -> p c t", t=4),
@@ -329,19 +332,19 @@ def tile_sae_t_kernel(tc, x, enc_w, enc_b, dec_w, dec_b, log_threshold, out_0, o
         x_transposes(1, 0)
         x_transposes(1, 1)
         quantise_x(0)
-        centre(1, 0)
         quantise_enc()
-        x_transposes(2, 0)
+        centre(1, 0)
         centre(1, 1)
         encode(0, 0)
         encode(0, 1)
+        x_transposes(2, 0)
         x_transposes(2, 1)
-        centre(2, 0)
         h_out(0, 0)
         h_out(0, 1)
         quantise_x(1)
         encode(0, 2)
         encode(0, 3)
+        centre(2, 0)
         centre(2, 1)
         h_out(0, 2)
         h_out(0, 3)

@@ -36,29 +36,34 @@ def tile_sae_t_kernel(tc, x, enc_w, enc_b, dec_w, dec_b, log_threshold, out_0, o
         psum = ctx.enter_context(tc.psum_pool(name="psum", bufs=2))
         ctx.enter_context(tc.manual_schedule())
 
+        x_sum_t = {}
         xs_t, xt_t, xc_t, xq_t, h_t, hf_t = {}, {}, {}, {}, {}, {}
         ap_t, ag_t, aq_t, st_t, ss_t, r_t, d_t = {}, {}, {}, {}, {}, {}, {}
 
         def live(q):
             return 0 <= q < ROUNDS
 
-        def load(q):
+        def load(q, part=None):
             if live(q):
-                xs_t[q] = work.tile([P, 4 * D], BF16, name="xs", tag="xs", bufs=7)
+                if part != 1:
+                    xs_t[q] = work.tile([P, 4 * D], BF16, name="xs", tag="xs", bufs=7)
                 rows = x[q * TOK : (q + 1) * TOK, :].rearrange("(p j) k -> p (j k)", j=4)
-                pieces = 2 if q == 0 else 1
-                for i in range(pieces):
+                pieces = 2 if q < 2 else 1
+                for i in range(pieces) if part is None else [part]:
                     cols = slice(i * 4 * D // pieces, (i + 1) * 4 * D // pieces)
                     nc.sync.dma_start(out=xs_t[q][:, cols], in_=rows[:, cols])
 
         warm = consts.tile([P, 1], F32, name="warm")
-        nc.vector.memset(warm[:], 0.0)
         warm2 = consts.tile([P, 1], F32, name="warm2")
-        nc.scalar.activation(out=warm2[:], in_=warm[:], func=ACT.Exp)
+        load(0)
+        decb4 = consts.tile([P, 4], BF16, name="decb4")
+        with nc.allow_non_contiguous_dma(reason="512 values, two to a piece"):
+            nc.scalar.dma_start(
+                out=decb4[:].rearrange("p (u e) -> p u e", u=2),
+                in_=dec_b.rearrange("(u p e) -> p u e", u=2, e=2),
+            )
         vb = consts.tile([P, P], BF16, name="vb")
         nc.vector.memset(vb[:], 0.0)
-        vw = consts.tile([P, 2 * P], BF16, name="vw")
-        nc.vector.memset(vw[:], 0.0)
         ones = consts.tile([P, P], F32, name="ones")
         nc.vector.memset(ones[:], 2.0 ** -31)
         ident_f = consts.tile([P, P], F32, name="ident_f")
@@ -66,18 +71,19 @@ def tile_sae_t_kernel(tc, x, enc_w, enc_b, dec_w, dec_b, log_threshold, out_0, o
         ident_b = consts.tile([P, P], BF16, name="ident_b")
         make_identity(nc, ident_b[:])
 
-        nc.scalar.dma_start(out=vw[0:2, :], in_=dec_b.rearrange("(u w) -> u w", u=2))
         nc.scalar.dma_start(out=vb[0:4, :], in_=enc_b.rearrange("(t p) -> t p", p=P))
         nc.scalar.dma_start(out=vb[4:8, :], in_=log_threshold.rearrange("(t p) -> t p", p=P))
         nc.scalar.dma_start(out=vb[8:12, :], in_=dec_b.rearrange("(t p) -> t p", p=P))
-        load(0)
+        nc.vector.memset(warm[:], 0.0)
+        nc.scalar.activation(out=warm2[:], in_=warm[:], func=ACT.Exp)
+        load(1, 0)
         ew = consts.tile([P, 4 * D], BF16, name="ew")
         for b in range(2):
             nc.sync.dma_start(
                 out=ew[:, 2 * b * D : 2 * (b + 1) * D].rearrange("r (t k) -> r t k", t=2),
                 in_=enc_w[2 * b * P : 2 * (b + 1) * P, :].rearrange("(t r) k -> r t k", r=P),
             )
-        load(1)
+        load(1, 1)
         load(2)
         dw = consts.tile([P, 4 * D], BF16, name="dw")
         nc.sync.dma_start(
@@ -87,11 +93,6 @@ def tile_sae_t_kernel(tc, x, enc_w, enc_b, dec_w, dec_b, log_threshold, out_0, o
         load(3)
         load(4)
 
-        pw = psum.tile([P, P], F32, name="pw", tag="r")
-        nc.tensor.transpose(pw[:], vw[:].bitcast(F32), ident_f[:])
-        decw2 = consts.tile([P, 2], F32, name="decw2")
-        nc.vector.tensor_copy(out=decw2[:], in_=pw[:, 0:2])
-        decb4 = decw2[:].bitcast(BF16)
         decbf = consts.tile([P, 4], F32, name="decbf")
         ones_b = consts.tile([P, 2], BF16, name="ones_b")
         nc.vector.memset(ones_b[:], 1.0)
@@ -117,9 +118,11 @@ def tile_sae_t_kernel(tc, x, enc_w, enc_b, dec_w, dec_b, log_threshold, out_0, o
             dstw = dst[:].bitcast(F32).rearrange("p (c u) -> p c u", u=2)
             copy(out=dstw[:, 2 * P * b : 2 * P * (b + 1), :], in_=bank[:].rearrange("p u c -> p c u"))
 
+        early_banks = {(0, 1): "x_sum", (1, 0): "r_sum", (1, 1): "st", (2, 1): "x_sum", (3, 1): "x_sum"}
+
         def x_transposes(q, b):
             if live(q):
-                xt_t[q, b] = psum.tile([P, 2, 2 * P], F32, name="xt", tag="x_sum" if q < 3 and b == 1 else "xt", bufs=1)
+                xt_t[q, b] = psum.tile([P, 2, 2 * P], F32, name="xt", tag=early_banks.get((q, b), "xt"), bufs=1)
                 word_transposes(xs_t[q], b, xt_t[q, b])
 
         def x_sums(q):
@@ -127,7 +130,7 @@ def tile_sae_t_kernel(tc, x, enc_w, enc_b, dec_w, dec_b, log_threshold, out_0, o
                 for i in range(4):
                     for j in range(4):
                         nc.tensor.matmul(
-                            x_sum[:, q, i, :],
+                            x_sum_t[0][:, q, i, :],
                             lhsT=xs_t[q][:, j * D + i * P : j * D + (i + 1) * P],
                             rhs=ones_b[:],
                             start=j == 0,
@@ -141,13 +144,13 @@ def tile_sae_t_kernel(tc, x, enc_w, enc_b, dec_w, dec_b, log_threshold, out_0, o
                 nc.vector.tensor_tensor(
                     out=xc_t[q][:, 8 * P * b : 8 * P * (b + 1)].rearrange("p (c u e) -> p c u e", u=2, e=2),
                     in0=xt_t[q, b][:].bitcast(BF16).rearrange("p u (c e) -> p c u e", e=2),
-                    in1=decb4.rearrange("p (u e) -> p u e", e=2).unsqueeze(1).to_broadcast([P, 2 * P, 2, 2]),
+                    in1=decb4[:].rearrange("p (u e) -> p u e", e=2).unsqueeze(1).to_broadcast([P, 2 * P, 2, 2]),
                     op=ALU.subtract,
                 )
 
         def quantise(src, tag):
-            codes = work.tile([P, TOK], U32, name=tag + "_codes", tag=tag + "_codes", bufs=4, align_bytes=64)
-            scales = work.tile([P, TOK], U8, name=tag + "_scales", tag=tag + "_scales", bufs=4, align_bytes=64)
+            codes = work.tile([P, TOK], U32, name=tag + "_codes", tag=tag + "_codes", bufs=5, align_bytes=64)
+            scales = work.tile([P, TOK], U8, name=tag + "_scales", tag=tag + "_scales", bufs=5, align_bytes=64)
             nc.vector.quantize_mx(out=codes[:].bitcast(FP8X4), scales=scales[:], in_=src[:])
             return codes, scales
 
@@ -172,7 +175,7 @@ def tile_sae_t_kernel(tc, x, enc_w, enc_b, dec_w, dec_b, log_threshold, out_0, o
                 mx(h_t[q, t], (enc_q, enc_s), t, xq_t[q])
 
         def h_out(q, t):
-            if live(q):
+            if live(q) and (q, t) not in hf_t:
                 hf_t[q, t] = work.tile([P, TOK], F32, name="hf", tag="hf", bufs=8)
                 nc.scalar.activation(
                     out=hf_t[q, t][:], in_=h_t[q, t][:], func=ACT.Relu, bias=encb[:, t : t + 1], scale=1.0
@@ -308,8 +311,44 @@ def tile_sae_t_kernel(tc, x, enc_w, enc_b, dec_w, dec_b, log_threshold, out_0, o
         def quantise_dec():
             nc.vector.quantize_mx(out=dec_q[:].bitcast(FP8X4), scales=dec_s[:], in_=dg[:])
 
+        x_transposes(0, 0)
+        x_transposes(0, 1)
+        centre(0, 0)
+        centre(0, 1)
+        x_transposes(1, 0)
+        enc_transposes(0)
+        enc_transposes(1)
+        centre(1, 0)
+        enc_out(0)
+        enc_out(1)
+        x_transposes(1, 1)
         vector_transpose()
+        quantise_x(0)
+        centre(1, 1)
         enc_b_out()
+        threshold()
+        quantise_enc()
+        x_transposes(2, 0)
+        x_transposes(2, 1)
+        centre(2, 0)
+        centre(2, 1)
+        encode(0, 0)
+        encode(0, 1)
+        x_transposes(3, 0)
+        x_transposes(3, 1)
+        quantise_x(1)
+        h_out(0, 0)
+        h_out(0, 1)
+        encode(0, 2)
+        encode(0, 3)
+        centre(3, 0)
+        h_out(0, 2)
+        h_out(0, 3)
+        encode(1, 0)
+        encode(1, 1)
+        dec_transposes(0)
+        dec_transposes(1)
+
         b_sq = consts.tile([P, 4], F32, name="b_sq")
         nc.vector.scalar_tensor_tensor(
             out=b_sq[:],
@@ -320,42 +359,8 @@ def tile_sae_t_kernel(tc, x, enc_w, enc_b, dec_w, dec_b, log_threshold, out_0, o
             op1=ALU.mult,
             accum_out=lacc[:, 2 * ROUNDS + 4 : 2 * ROUNDS + 5],
         )
-        threshold()
-        x_transposes(0, 0)
-        x_transposes(0, 1)
-        centre(0, 0)
-        centre(0, 1)
-        enc_transposes(0)
-        enc_transposes(1)
-        enc_out(0)
-        enc_out(1)
-        x_transposes(1, 0)
-        x_transposes(1, 1)
-        quantise_x(0)
-        quantise_enc()
-        centre(1, 0)
-        centre(1, 1)
-        encode(0, 0)
-        encode(0, 1)
-        x_transposes(2, 0)
-        x_transposes(2, 1)
-        h_out(0, 0)
-        h_out(0, 1)
-        quantise_x(1)
-        encode(0, 2)
-        encode(0, 3)
-        centre(2, 0)
-        centre(2, 1)
-        h_out(0, 2)
-        h_out(0, 3)
-        encode(1, 0)
-        encode(1, 1)
-        dec_transposes(0)
-        dec_transposes(1)
-        x_transposes(3, 0)
 
         r_sum = psum.tile([P, D], F32, name="r_sum", tag="r_sum", bufs=1)
-        x_sum = psum.tile([P, ROUNDS, 4, 2], F32, name="x_sum", tag="x_sum", bufs=1)
 
         def first_round():
             h_out(1, 0)
@@ -364,6 +369,8 @@ def tile_sae_t_kernel(tc, x, enc_w, enc_b, dec_w, dec_b, log_threshold, out_0, o
             encode(1, 3)
             jump(0, 0)
             jump(0, 1)
+            centre(3, 1)
+            x_sum_t[0] = psum.tile([P, ROUNDS, 4, 2], F32, name="x_sum", tag="x_sum", bufs=1)
             quantise_x(2)
             jump(0, 2)
             jump(0, 3)
@@ -371,21 +378,19 @@ def tile_sae_t_kernel(tc, x, enc_w, enc_b, dec_w, dec_b, log_threshold, out_0, o
             dec_out(1, nc.scalar.copy)
             h_out(1, 2)
             h_out(1, 3)
-            centre(3, 0)
             a_transposes(0, 0)
-            x_transposes(3, 1)
+            x_transposes(4, 0)
+            quantise_x(3)
             regroup(0)
             s_out(0, 0)
             encode(2, 0)
             encode(2, 1)
-            centre(3, 1)
             x_sums(0)
             a_transposes(0, 1)
-            x_transposes(4, 0)
             h_out(2, 0)
+            h_out(2, 1)
             s_out(0, 1)
             quantise_dec()
-            quantise_x(3)
             quantise_a(0)
             decode(0, 0)
             decode(0, 1)
@@ -473,7 +478,7 @@ def tile_sae_t_kernel(tc, x, enc_w, enc_b, dec_w, dec_b, log_threshold, out_0, o
         junk = consts.tile([P, D], F32, name="junk")
         nc.vector.scalar_tensor_tensor(
             out=junk[:, 0 : 4 * ROUNDS].rearrange("p (q i) -> p q i", i=4),
-            in0=x_sum[:, :, :, 0],
+            in0=x_sum_t[0][:, :, :, 0],
             scalar=-128.0,
             in1=decbf[:].unsqueeze(1).to_broadcast([P, ROUNDS, 4]),
             op0=ALU.mult,

from contextlib import ExitStack

import concourse.mybir as mybir
from concourse.masks import make_identity

FLOPS = 2 * 2 * 8192 * 512 * 512

F32 = mybir.dt.float32
BF16 = mybir.dt.bfloat16
U32 = mybir.dt.uint32
U8 = mybir.dt.uint8
FP8X4 = mybir.dt.float8_e4m3fn_x4
ALU = mybir.AluOpType
ACT = mybir.ActivationFunctionType
AX = mybir.AxisListType

P = 128
D = 512
TOK = 512
N_TOK = 8192
ROUNDS = N_TOK // TOK


def as_row(ap):
    v = ap
    while v.ndim < 2:
        v = v.unsqueeze(0)
    return v


def tile_sae_t_kernel(tc, x, enc_w, enc_b, dec_w, dec_b, log_threshold, out_0, out_1):
    nc = tc.nc
    with ExitStack() as ctx:
        consts = ctx.enter_context(tc.tile_pool(name="consts", bufs=1))
        work = ctx.enter_context(tc.tile_pool(name="work", bufs=2))
        psum = ctx.enter_context(tc.psum_pool(name="psum", bufs=2))
        ctx.enter_context(tc.manual_schedule())

        x_sum_t = {}
        xs_t, xt_t, xc_t, xq_t, h_t, hf_t = {}, {}, {}, {}, {}, {}
        ap_t, ag_t, aq_t, st_t, ss_t, r_t, d_t = {}, {}, {}, {}, {}, {}, {}

        def live(q):
            return 0 <= q < ROUNDS

        def load(q, part=None):
            if live(q):
                if part != 1:
                    xs_t[q] = work.tile([P, 4 * D], BF16, name="xs", tag="xs", bufs=7)
                rows = x[q * TOK : (q + 1) * TOK, :].rearrange("(p j) k -> p (j k)", j=4)
                pieces = 2 if q < 2 else 1
                for i in range(pieces) if part is None else [part]:
                    cols = slice(i * 4 * D // pieces, (i + 1) * 4 * D // pieces)
                    nc.sync.dma_start(out=xs_t[q][:, cols], in_=rows[:, cols])

        warm = consts.tile([P, 1], F32, name="warm")
        warm2 = consts.tile([P, 1], F32, name="warm2")
        load(0)
        decb4 = consts.tile([P, 4], BF16, name="decb4")
        with nc.allow_non_contiguous_dma(reason="512 values, two to a piece"):
            nc.scalar.dma_start(
                out=decb4[:].rearrange("p (u e) -> p u e", u=2),
                in_=dec_b.rearrange("(u p e) -> p u e", u=2, e=2),
            )
        vb = consts.tile([P, P], BF16, name="vb")
        nc.vector.memset(vb[:], 0.0)
        ones = consts.tile([P, P], F32, name="ones")
        nc.vector.memset(ones[:], 2.0 ** -31)
        ident_f = consts.tile([P, P], F32, name="ident_f")
        make_identity(nc, ident_f[:])
        ident_b = consts.tile([P, P], BF16, name="ident_b")
        make_identity(nc, ident_b[:])

        nc.scalar.dma_start(out=vb[0:4, :], in_=enc_b.rearrange("(t p) -> t p", p=P))
        nc.scalar.dma_start(out=vb[4:8, :], in_=log_threshold.rearrange("(t p) -> t p", p=P))
        nc.scalar.dma_start(out=vb[8:12, :], in_=dec_b.rearrange("(t p) -> t p", p=P))
        nc.vector.memset(warm[:], 0.0)
        nc.scalar.activation(out=warm2[:], in_=warm[:], func=ACT.Exp)
        load(1, 0)
        ew = consts.tile([P, 4 * D], BF16, name="ew")
        for b in range(2):
            nc.sync.dma_start(
                out=ew[:, 2 * b * D : 2 * (b + 1) * D].rearrange("r (t k) -> r t k", t=2),
                in_=enc_w[2 * b * P : 2 * (b + 1) * P, :].rearrange("(t r) k -> r t k", r=P),
            )
        load(1, 1)
        load(2)
        dw = consts.tile([P, 4 * D], BF16, name="dw")
        nc.sync.dma_start(
            out=dw[:].rearrange("r (c h) -> r c h", c=4),
            in_=dec_w.rearrange("(c r) h -> r c h", r=P),
        )
        load(3)
        load(4)

        decbf = consts.tile([P, 4], F32, name="decbf")
        ones_b = consts.tile([P, 2], BF16, name="ones_b")
        nc.vector.memset(ones_b[:], 1.0)
        btab = consts.tile([P, D], BF16, name="btab")
        lacc = consts.tile([P, 2 * ROUNDS + 5], F32, name="lacc")
        encb = consts.tile([P, 4], F32, name="encb")
        thr = consts.tile([P, 4], F32, name="thr")
        enc_q = consts.tile([P, D], U32, name="enc_q", align_bytes=64)
        enc_s = consts.tile([P, D], U8, name="enc_s", align_bytes=64)
        dec_q = consts.tile([P, D], U32, name="dec_q", align_bytes=64)
        dec_s = consts.tile([P, D], U8, name="dec_s", align_bytes=64)
        eg = consts.tile([P, 4 * D], BF16, name="eg", align_bytes=64)
        dg = consts.tile([P, 4 * D], BF16, name="dg", align_bytes=64)

        def word_transposes(src, b, bank):
            srcw = src[:].bitcast(F32)
            for jj in range(2):
                for u in range(2):
                    c0 = (2 * b + jj) * 256 + P * u
                    nc.tensor.transpose(bank[:, u, P * jj : P * jj + P], srcw[:, c0 : c0 + P], ident_f[:])

        def words_out(copy, bank, dst, b):
            dstw = dst[:].bitcast(F32).rearrange("p (c u) -> p c u", u=2)
            copy(out=dstw[:, 2 * P * b : 2 * P * (b + 1), :], in_=bank[:].rearrange("p u c -> p c u"))

        early_banks = {(0, 1): "x_sum", (1, 0): "r_sum", (1, 1): "st", (2, 1): "x_sum", (3, 1): "x_sum"}

        def x_transposes(q, b):
            if live(q):
                xt_t[q, b] = psum.tile([P, 2, 2 * P], F32, name="xt", tag=early_banks.get((q, b), "xt"), bufs=1)
                word_transposes(xs_t[q], b, xt_t[q, b])

        def x_sums(q):
            if live(q):
                for i in range(4):
                    for j in range(4):
                        nc.tensor.matmul(
                            x_sum_t[0][:, q, i, :],
                            lhsT=xs_t[q][:, j * D + i * P : j * D + (i + 1) * P],
                            rhs=ones_b[:],
                            start=j == 0,
                            stop=j == 3,
                        )

        def centre(q, b):
            if live(q):
                if q not in xc_t:
                    xc_t[q] = work.tile([P, 4 * TOK], BF16, name="xc", tag="xc", bufs=2, align_bytes=64)
                nc.vector.tensor_tensor(
                    out=xc_t[q][:, 8 * P * b : 8 * P * (b + 1)].rearrange("p (c u e) -> p c u e", u=2, e=2),
                    in0=xt_t[q, b][:].bitcast(BF16).rearrange("p u (c e) -> p c u e", e=2),
                    in1=decb4[:].rearrange("p (u e) -> p u e", e=2).unsqueeze(1).to_broadcast([P, 2 * P, 2, 2]),
                    op=ALU.subtract,
                )

        def quantise(src, tag):
            codes = work.tile([P, TOK], U32, name=tag + "_codes", tag=tag + "_codes", bufs=5, align_bytes=64)
            scales = work.tile([P, TOK], U8, name=tag + "_scales", tag=tag + "_scales", bufs=5, align_bytes=64)
            nc.vector.quantize_mx(out=codes[:].bitcast(FP8X4), scales=scales[:], in_=src[:])
            return codes, scales

        def quantise_x(q):
            if live(q):
                xq_t[q] = quantise(xc_t[q], "x")

        def mx(bank, stationary, i, moving, start=True, stop=True):
            nc.tensor.matmul_mx(
                out=bank[:],
                lhsT=stationary[0][:, i * P : (i + 1) * P].bitcast(FP8X4),
                lhsT_scale=stationary[1][:, i * P : (i + 1) * P],
                rhs=moving[0][:].bitcast(FP8X4),
                rhs_scale=moving[1][:],
                start=start,
                stop=stop,
            )

        def encode(q, t):
            if live(q):
                h_t[q, t] = psum.tile([P, TOK], F32, name="hps", tag="r" if q == 0 and t >= 2 else "h")
                mx(h_t[q, t], (enc_q, enc_s), t, xq_t[q])

        def h_out(q, t):
            if live(q) and (q, t) not in hf_t:
                hf_t[q, t] = work.tile([P, TOK], F32, name="hf", tag="hf", bufs=8)
                nc.scalar.activation(
                    out=hf_t[q, t][:], in_=h_t[q, t][:], func=ACT.Relu, bias=encb[:, t : t + 1], scale=1.0
                )

        def jump(q, t):
            if live(q):
                if t == 0:
                    ap_t[q] = work.tile([P, 4 * TOK], BF16, name="ap", tag="ap", bufs=3)
                nc.vector.scalar_tensor_tensor(
                    out=ap_t[q][:, t * TOK : (t + 1) * TOK],
                    in0=hf_t[q, t][:],
                    scalar=thr[:, t : t + 1],
                    in1=hf_t[q, t][:],
                    op0=ALU.is_gt,
                    op1=ALU.mult,
                )

        def regroup(q):
            if live(q):
                ag_t[q] = work.tile([P, 4 * TOK], BF16, name="ag", tag="ag", bufs=2, align_bytes=64)
                if q == 0 or q >= ROUNDS - 3:
                    split = TOK // 32 if q == ROUNDS - 1 else 0
                    grouped = ag_t[q][:].rearrange("p (c i t) -> p c t i", i=4, t=4)
                    plain = ap_t[q][:].rearrange("p (t c i) -> p c t i", t=4, i=4)
                    nc.vector.tensor_copy(out=grouped[:, split:, :, :], in_=plain[:, split:, :, :])
                    if split:
                        nc.scalar.copy(out=grouped[:, 0:split, :, :], in_=plain[:, 0:split, :, :])
                else:
                    nc.gpsimd.tensor_scalar(
                        out=ag_t[q][:].rearrange("p (c t) -> p c t", t=4),
                        in0=ap_t[q][:].rearrange("p (t c) -> p c t", t=4),
                        scalar1=1.0,
                        scalar2=0.0,
                        op0=ALU.mult,
                        op1=ALU.add,
                    )

        def quantise_a(q):
            if live(q):
                aq_t[q] = quantise(ag_t[q], "a")

        def a_transposes(q, b):
            if live(q):
                st_t[q, b] = psum.tile([P, 2, D], BF16, name="st", tag="xt" if q == ROUNDS - 1 and b else "st", bufs=1)
                for jj in range(2):
                    for t in range(4):
                        c0 = t * TOK + (2 * b + jj) * P
                        nc.tensor.transpose(
                            st_t[q, b][:, jj, t * P : (t + 1) * P], ap_t[q][:, c0 : c0 + P], ident_b[:]
                        )

        def s_out(q, b):
            if live(q):
                if b == 0:
                    ss_t[q] = work.tile([P, 4 * D], F32, name="ssb", tag="ssb", bufs=3)
                s_half = ss_t[q][:, 2 * b * D : (2 * b + 2) * D]
                a_half = st_t[q, b][:].rearrange("p j h -> p (j h)")
                nc.scalar.activation(out=s_half, in_=a_half, func=ACT.Sign)
                rows = out_0[q * TOK : (q + 1) * TOK, :].rearrange("(p j) h -> p (j h)", j=4)
                if q == ROUNDS - 1:
                    nc.sync.dma_start(out=rows[:, 2 * b * D : (2 * b + 2) * D], in_=s_half)
                elif b == 1:
                    nc.sync.dma_start(out=rows, in_=ss_t[q][:])

        def decode(q, j):
            if live(q):
                r_t[q, j] = psum.tile([P, D], F32, name="rps", tag="h" if q >= ROUNDS - 2 and j >= 2 else "xt" if q >= ROUNDS - 4 and j == 2 else "r", bufs=1 if ROUNDS - 4 <= q < ROUNDS - 2 and j == 2 else 2)
                mx(r_t[q, j], aq_t[q], j, (dec_q, dec_s))

        def add_up(q, j):
            if live(q):
                mx(r_sum, aq_t[q], j, (dec_q, dec_s), start=q + j == 0, stop=q == ROUNDS - 1 and j == 3)

        def residual(q, j):
            if live(q):
                if j == 0:
                    d_t[q] = work.tile([P, 4 * D], F32, name="d0", tag="d0", bufs=2)
                nc.vector.scalar_tensor_tensor(
                    out=d_t[q][:, j * D : (j + 1) * D],
                    in0=xs_t[q][:, j * D : (j + 1) * D],
                    scalar=-64.0,
                    in1=r_t[q, j][:],
                    op0=ALU.mult,
                    op1=ALU.add,
                )

        def square(q, half):
            if live(q):
                square_columns(q, 2 * half, 2, 2 * q + half)

        def square_columns(q, j, n, column):
            d = d_t[q][:, j * D : (j + n) * D]
            nc.scalar.activation(out=d, in_=d, func=ACT.Square, accum_out=lacc[:, column : column + 1])

        e_banks = []
        d_banks = []
        pv = psum.tile([P, P], BF16, name="pv", tag="r")
        dgv = dg[:].rearrange("p (c j t) -> p c j t", c=4, t=4)

        def enc_transposes(b):
            et = psum.tile([P, 2, 2 * P], F32, name="et", tag="h")
            word_transposes(ew, b, et)
            e_banks.append(et)

        def enc_out(b):
            words_out(nc.scalar.copy, e_banks[b], eg, b)

        def quantise_enc():
            nc.vector.quantize_mx(out=enc_q[:].bitcast(FP8X4), scales=enc_s[:], in_=eg[:])

        def vector_transpose():
            nc.tensor.transpose(pv[:], vb[:], ident_b[:])

        def enc_b_out():
            nc.vector.tensor_copy(out=encb[:], in_=pv[:, 0:4])
            nc.vector.tensor_copy(out=decbf[:], in_=pv[:, 8:12])

        def threshold():
            nc.scalar.activation(out=thr[:], in_=pv[:, 4:8], func=ACT.Exp)

        def dec_transposes(cb):
            dt = psum.tile([P, 2, 4, P], BF16, name="dt", tag="r_sum" if cb else "st", bufs=1)
            for cc in range(2):
                for t in range(4):
                    c0 = (2 * cb + cc) * D + P * t
                    nc.tensor.transpose(dt[:, cc, t, :], dw[:, c0 : c0 + P], ident_b[:])
            d_banks.append(dt)

        def dec_out(cb, copy):
            copy(out=dgv[:, 2 * cb : 2 * cb + 2, :, :], in_=d_banks[cb][:].rearrange("p c t j -> p c j t"))

        def quantise_dec():
            nc.vector.quantize_mx(out=dec_q[:].bitcast(FP8X4), scales=dec_s[:], in_=dg[:])

        x_transposes(0, 0)
        x_transposes(0, 1)
        centre(0, 0)
        centre(0, 1)
        x_transposes(1, 0)
        enc_transposes(0)
        enc_transposes(1)
        centre(1, 0)
        enc_out(0)
        enc_out(1)
        x_transposes(1, 1)
        vector_transpose()
        quantise_x(0)
        centre(1, 1)
        enc_b_out()
        threshold()
        quantise_enc()
        x_transposes(2, 0)
        x_transposes(2, 1)
        centre(2, 0)
        centre(2, 1)
        encode(0, 0)
        encode(0, 1)
        x_transposes(3, 0)
        x_transposes(3, 1)
        quantise_x(1)
        h_out(0, 0)
        h_out(0, 1)
        encode(0, 2)
        encode(0, 3)
        centre(3, 0)
        h_out(0, 2)
        h_out(0, 3)
        encode(1, 0)
        encode(1, 1)
        dec_transposes(0)
        dec_transposes(1)

        b_sq = consts.tile([P, 4], F32, name="b_sq")
        nc.vector.scalar_tensor_tensor(
            out=b_sq[:],
            in0=decbf[:],
            scalar=float(N_TOK),
            in1=decbf[:],
            op0=ALU.mult,
            op1=ALU.mult,
            accum_out=lacc[:, 2 * ROUNDS + 4 : 2 * ROUNDS + 5],
        )

        r_sum = psum.tile([P, D], F32, name="r_sum", tag="r_sum", bufs=1)

        def first_round():
            h_out(1, 0)
            h_out(1, 1)
            encode(1, 2)
            encode(1, 3)
            jump(0, 0)
            jump(0, 1)
            centre(3, 1)
            x_sum_t[0] = psum.tile([P, ROUNDS, 4, 2], F32, name="x_sum", tag="x_sum", bufs=1)
            quantise_x(2)
            jump(0, 2)
            jump(0, 3)
            dec_out(0, nc.scalar.copy)
            dec_out(1, nc.scalar.copy)
            h_out(1, 2)
            h_out(1, 3)
            a_transposes(0, 0)
            x_transposes(4, 0)
            quantise_x(3)
            regroup(0)
            s_out(0, 0)
            encode(2, 0)
            encode(2, 1)
            x_sums(0)
            a_transposes(0, 1)
            h_out(2, 0)
            h_out(2, 1)
            s_out(0, 1)
            quantise_dec()
            quantise_a(0)
            decode(0, 0)
            decode(0, 1)

        def steady_round(q):
            h_out(q + 1, 1)
            add_up(q - 1, 0)
            encode(q + 1, 2)
            encode(q + 1, 3)
            square(q - 2, 1)
            jump(q, 0)
            jump(q, 1)
            jump(q, 2)
            jump(q, 3)
            h_out(q + 1, 2)
            h_out(q + 1, 3)
            centre(q + 3, 0)
            a_transposes(q, 0)
            x_transposes(q + 3, 1)
            residual(q - 1, 0)
            regroup(q)
            residual(q - 1, 1)
            s_out(q, 0)
            square(q - 1, 0)
            decode(q - 1, 2)
            decode(q - 1, 3)
            centre(q + 3, 1)
            encode(q + 2, 0)
            encode(q + 2, 1)
            x_sums(q)
            a_transposes(q, 1)
            x_transposes(q + 4, 0)
            residual(q - 1, 2)
            residual(q - 1, 3)
            h_out(q + 2, 0)
            s_out(q, 1)
            add_up(q - 1, 1)
            add_up(q - 1, 2)
            add_up(q - 1, 3)
            quantise_x(q + 3)
            quantise_a(q)
            decode(q, 0)
            decode(q, 1)

        def last_round():
            q = ROUNDS - 1
            decode(q - 1, 2)
            decode(q - 1, 3)
            square(q - 2, 1)
            for t in range(4):
                jump(q, t)
            a_transposes(q, 0)
            a_transposes(q, 1)
            residual(q - 1, 0)
            regroup(q)
            s_out(q, 0)
            residual(q - 1, 1)
            square(q - 1, 0)
            quantise_a(q)
            residual(q - 1, 2)
            residual(q - 1, 3)
            s_out(q, 1)
            for j in range(4):
                add_up(q - 1, j)
            square(q - 1, 1)
            x_sums(q)
            for j in range(4):
                decode(q, j)
            for j in range(4):
                add_up(q, j)
            for j in range(3):
                residual(q, j)
                square_columns(q, j, 1, 2 * q + j)
            residual(q, 3)

        load(5)
        first_round()
        for q in range(1, ROUNDS - 1):
            load(q + 5)
            if q == 3:
                nc.sync.dma_start(out=btab[:], in_=dec_b.partition_broadcast(P))
            steady_round(q)
        last_round()

        junk = consts.tile([P, D], F32, name="junk")
        nc.vector.scalar_tensor_tensor(
            out=junk[:, 0 : 4 * ROUNDS].rearrange("p (q i) -> p q i", i=4),
            in0=x_sum_t[0][:, :, :, 0],
            scalar=-128.0,
            in1=decbf[:].unsqueeze(1).to_broadcast([P, ROUNDS, 4]),
            op0=ALU.mult,
            op1=ALU.mult,
            accum_out=lacc[:, 2 * ROUNDS + 2 : 2 * ROUNDS + 3],
        )
        junk2 = consts.tile([P, D], F32, name="junk2")
        nc.vector.scalar_tensor_tensor(
            out=junk2[:],
            in0=r_sum[:],
            scalar=2.0,
            in1=btab[:],
            op0=ALU.mult,
            op1=ALU.mult,
            accum_out=lacc[:, 2 * ROUNDS + 3 : 2 * ROUNDS + 4],
        )
        d = d_t[ROUNDS - 1][:, 3 * D : 4 * D]
        nc.vector.scalar_tensor_tensor(
            out=junk[:],
            in0=d,
            scalar=1.0,
            in1=d,
            op0=ALU.mult,
            op1=ALU.mult,
            accum_out=lacc[:, 2 * ROUNDS + 1 : 2 * ROUNDS + 2],
        )

        pl = psum.tile([P, 2 * ROUNDS + 5], F32, name="pl", tag="r")
        nc.tensor.matmul(pl[:], lhsT=ones[:], rhs=lacc[:], start=True, stop=True)
        tot = consts.tile([P, 1], F32, name="tot")
        nc.vector.tensor_reduce(out=tot[:], in_=pl[:], axis=AX.X, op=ALU.add)
        nc.sync.dma_start(out=as_row(out_1), in_=tot[0:1, 0:1])
